import numpy as np
import ml_dtypes


def mxq(x, axis, fmt="e4m3"):
    dtype, down = {"e4m3": (ml_dtypes.float8_e4m3fn, 7), "e5m2": (ml_dtypes.float8_e5m2, 14)}[fmt]
    v = np.moveaxis(np.asarray(x, np.float32).astype(ml_dtypes.bfloat16).astype(np.float64), axis, -1)
    blocks = v.reshape(v.shape[:-1] + (-1, 32))
    amax = np.abs(blocks).max(-1, keepdims=True)
    byte = np.maximum(np.where(amax > 0, np.frexp(amax)[1] - 1 + 127, 0) - down, 1)
    scale = np.exp2(byte - 127.0)
    codes = (blocks / scale).astype(np.float32).astype(dtype).astype(np.float64)
    return np.moveaxis((codes * scale).reshape(v.shape), -1, axis)


WIDE = False


def mx_kscale(k):
    if not WIDE:
        return np.ones(k)
    levels = np.array([10, -10, 5, -5, 0])
    a = np.random.permutation(np.resize(levels, k // 512 * 4)).reshape(k // 512, 4)
    idx = np.arange(k)
    return np.exp2(a[idx // 512, idx % 128 // 32])


BF16 = ml_dtypes.bfloat16


def bf(x):
    return np.asarray(x, np.float32).astype(BF16)


def f64(x):
    return np.asarray(x).astype(np.float64)


E2M1 = np.array([0.0, 0.5, 1.0, 1.5, 2.0, 3.0, 4.0, 6.0, -0.0, -0.5, -1.0, -1.5, -2.0, -3.0, -4.0, -6.0])


def pack_weight(w, fmt):
    k, n = w.shape
    w = f64(bf(w)).reshape(k // 32, 32, n)
    amax = np.abs(w).max(1)
    if fmt == "e4m3":
        byte = np.frexp(amax)[1] - 1 + 127 - 7
    else:
        mant, ex = np.frexp(amax / 6.0)
        byte = np.where(mant > 0.5, ex, ex - 1) + 127
    byte = np.clip(np.where(amax > 0, byte, 1), 1, 254)
    scaled = (w * np.exp2(127.0 - byte)[:, None, :]).reshape(k, n).astype(np.float32)
    by_word = np.ascontiguousarray(scaled.reshape(k // 512, 128, 4, n).transpose(0, 1, 3, 2))
    if fmt == "e4m3":
        words = by_word.astype(ml_dtypes.float8_e4m3fn).view(np.uint8)
    else:
        c = by_word.astype(ml_dtypes.float4_e2m1fn).view(np.uint8) & 0xF
        words = c[..., 0::2] | (c[..., 1::2] << 4)
    return np.ascontiguousarray(words), np.ascontiguousarray(byte.astype(np.uint8).reshape(k // 512, 16, n))


def unpack_weight(words, scales, fmt):
    g, p, n, _ = words.shape
    if fmt == "e4m3":
        vals = np.ascontiguousarray(words).view(ml_dtypes.float8_e4m3fn).astype(np.float64)
    else:
        nib = np.empty((g, p, n, 4), np.uint8)
        nib[..., 0::2] = words & 0xF
        nib[..., 1::2] = words >> 4
        vals = E2M1[nib]
    vals = vals * np.repeat(np.exp2(scales.astype(np.float64) - 127.0), 8, axis=1)[..., None]
    return vals.transpose(0, 1, 3, 2).reshape(g * 512, n)


B, SY, SX, D, F = 2, 128, 2048, 512, 16384
EPS = 1e-5
FMT = "e4m3"


def layer_norm_all(t):
    mu = t.mean()
    var = np.square(t - mu).mean()
    return (t - mu) / np.sqrt(var + EPS)


def setup_inputs():
    t = mx_kscale(F)
    h2 = bf(np.random.standard_normal((B, SY, D)))
    w_ff1 = np.random.standard_normal((F, D)) / np.sqrt(D) * t[:, None]
    w_ff1_words, w_ff1_scales = pack_weight(np.ascontiguousarray(w_ff1.T), FMT)
    b_ff1 = bf(np.random.standard_normal(F) * 0.3 * t)
    w_ff2 = np.random.standard_normal((D, F)) * 1.4 / np.sqrt(F) / t[None, :]
    w_ff2_words, w_ff2_scales = pack_weight(np.ascontiguousarray(w_ff2.T), FMT)
    b_ff2 = bf(0.2 + 0.2 * np.random.standard_normal(D))
    return {"h2": h2,
            "w_ff1_words": w_ff1_words,
            "w_ff1_scales": w_ff1_scales,
            "b_ff1": b_ff1,
            "w_ff2_words": w_ff2_words,
            "w_ff2_scales": w_ff2_scales,
            "b_ff2": b_ff2}


def reference(h2, w_ff1_words, w_ff1_scales, b_ff1, w_ff2_words, w_ff2_scales, b_ff2):
    h = f64(h2)
    a = np.maximum((mxq(h, 2, "e4m3") @ unpack_weight(w_ff1_words, w_ff1_scales, FMT)) + f64(b_ff1), 0.0)
    ff = (mxq(a, 2, "e4m3") @ unpack_weight(w_ff2_words, w_ff2_scales, FMT)) + f64(b_ff2)
    return layer_norm_all(h + ff)

@@ -1,0 +1,313 @@
+from contextlib import ExitStack
+
+import concourse.mybir as mybir
+from concourse.masks import make_identity
+
+F32 = mybir.dt.float32
+BF16 = mybir.dt.bfloat16
+I32 = mybir.dt.int32
+U32 = mybir.dt.uint32
+U8 = mybir.dt.uint8
+FP8X4 = mybir.dt.float8_e4m3fn_x4
+ALU = mybir.AluOpType
+ACT = mybir.ActivationFunctionType
+
+P = 128
+PACK = 4
+K_PASS = P * PACK
+HALVES = 2
+PAIR = 2
+TOKEN_TILES = 2
+TOKENS = TOKEN_TILES * P
+D = 512
+F = 16384
+PASSES = F // K_PASS
+PLANES = 4
+ROUND = 2
+ROUNDS = PASSES // ROUND
+EPS = 1e-5
+
+FLOPS = 2 * TOKENS * D * F * 2
+
+
+def tile_decoderblock_pb_k_kernel(
+    tc, h2, w_ff1_words, w_ff1_scales, b_ff1, w_ff2_words, w_ff2_scales, b_ff2, out
+):
+    nc = tc.nc
+    with ExitStack() as ctx:
+        keep = ctx.enter_context(tc.tile_pool(name="keep", bufs=1))
+        work = ctx.enter_context(tc.tile_pool(name="work", bufs=2))
+        psum_ff = ctx.enter_context(tc.psum_pool(name="psum_ff", bufs=1))
+        psum_x = ctx.enter_context(tc.psum_pool(name="psum_x", bufs=ROUND * TOKEN_TILES))
+        psum_t = ctx.enter_context(tc.psum_pool(name="psum_t", bufs=ROUND))
+        ctx.enter_context(tc.manual_schedule())
+
+        h_tok = keep.tile([P, TOKEN_TILES, D], BF16)
+        nc.sync.dma_start(out=h_tok[:], in_=h2.rearrange("i p d -> p i d"))
+
+        bias_rows = keep.tile([P, K_PASS], BF16)
+        nc.vector.memset(bias_rows[:], 0.0)
+        nc.sync.dma_start(
+            out=bias_rows[0:PASSES, :], in_=b_ff1.rearrange("(g c) -> g c", c=K_PASS)
+        )
+        nc.sync.dma_start(
+            out=bias_rows[PASSES : PASSES + 1, :], in_=b_ff2.rearrange("(o c) -> o c", o=1)
+        )
+
+        w1_planes = keep.tile([P, F // PLANES], U8, align_bytes=64)
+        nc.vector.memset(w1_planes[:].bitcast(I32), 0)
+        for quadrant in range(4):
+            nc.sync.dma_start(
+                out=w1_planes[32 * quadrant : 32 * quadrant + 4 * PLANES, :].bitcast(I32),
+                in_=w_ff1_scales[0, 4 * quadrant : 4 * quadrant + 4, :]
+                .rearrange("r (j c) -> j r c", j=PLANES)
+                .bitcast(I32),
+            )
+
+        w2_planes = keep.tile([P, PASSES, D], U8, align_bytes=64)
+        nc.vector.memset(w2_planes[:].rearrange("p g n -> p (g n)").bitcast(I32), 0)
+
+        w1_words = keep.tile([P, F], U32, align_bytes=64)
+        w2_words = keep.tile([P, PASSES, D], U32, align_bytes=64)
+        w1_dram = w_ff1_words[0].rearrange("p n t -> p (n t)").bitcast(I32)
+        w2_dram = w_ff2_words.rearrange("g p n t -> p g (n t)").bitcast(I32)
+
+        def load_w1(r):
+            cols = slice(r * ROUND * K_PASS, (r + 1) * ROUND * K_PASS)
+            nc.sync.dma_start(out=w1_words[:, cols].bitcast(I32), in_=w1_dram[:, cols])
+
+        def load_w2(r):
+            some = slice(r * ROUND, (r + 1) * ROUND)
+            nc.sync.dma_start(out=w2_words[:, some, :].bitcast(I32), in_=w2_dram[:, some, :])
+
+        load_w1(0)
+        load_w1(1)
+        for quadrant in range(4):
+            nc.sync.dma_start(
+                out=w2_planes[32 * quadrant : 32 * quadrant + 4, :, :].bitcast(I32),
+                in_=w_ff2_scales[:, 4 * quadrant : 4 * quadrant + 4, :]
+                .rearrange("g r n -> r g n")
+                .bitcast(I32),
+            )
+        for r in range(ROUNDS):
+            load_w2(r)
+            if r + 2 < ROUNDS:
+                load_w1(r + 2)
+
+        ident_f32 = keep.tile([P, P], F32)
+        make_identity(nc, ident_f32[:])
+        ident_bf16 = keep.tile([P, P], BF16)
+        make_identity(nc, ident_bf16[:])
+        neg_average = keep.tile([P, P], F32)
+        nc.vector.memset(neg_average[:], -1.0 / (TOKENS * D))
+        eps_col = keep.tile([P, 1], F32)
+        nc.vector.memset(eps_col[:], EPS)
+        warm_sqrt = keep.tile([P, 1], F32)
+        nc.scalar.activation(out=warm_sqrt[:], in_=eps_col[:], func=ACT.Sqrt)
+
+        def token_tile(i):
+            return slice(i * P, (i + 1) * P)
+
+        hT = psum_t.tile([P, HALVES, TOKENS], F32, tag="aT")
+        for i in range(TOKEN_TILES):
+            h_halves = h_tok[:, i, :].bitcast(F32)
+            for u in range(HALVES):
+                nc.tensor.transpose(
+                    hT[:, u, token_tile(i)], h_halves[:, u : D // PAIR : HALVES], ident_f32[:]
+                )
+        h_grouped = keep.tile([P, TOKENS * PACK], BF16, align_bytes=64)
+        nc.vector.tensor_copy(
+            out=h_grouped[:].bitcast(F32).rearrange("p (t u) -> p t u", u=HALVES),
+            in_=hT[:].rearrange("p u t -> p t u"),
+        )
+        h_codes = keep.tile([P, TOKENS], U32, align_bytes=64)
+        h_scales = keep.tile([P, TOKENS], U8, align_bytes=64)
+        nc.vector.quantize_mx(
+            out=h_codes[:].bitcast(FP8X4), scales=h_scales[:], in_=h_grouped[:]
+        )
+
+        def spread_row(row):
+            bank = psum_x.tile([P, K_PASS], F32, tag="x")
+            nc.tensor.matmul(
+                out=bank[:],
+                lhsT=ident_bf16[:, row : row + 1].to_broadcast([P, P]),
+                rhs=bias_rows[:],
+                start=True,
+                stop=True,
+            )
+            return bank
+
+        def by_halves(ap):
+            return ap.rearrange("q (p u e) -> q u p e", u=HALVES, e=PAIR)
+
+        def halves_apart(ap):
+            return ap.rearrange("q (u p e) -> q u p e", u=HALVES, e=PAIR)
+
+        bias_all = keep.tile([P, PASSES, K_PASS], BF16)
+        for g in range(PASSES):
+            bank = spread_row(g)
+            if g % 2 == 0:
+                nc.vector.tensor_copy(out=halves_apart(bias_all[:, g, :]), in_=by_halves(bank[:]))
+            else:
+                nc.scalar.copy(out=halves_apart(bias_all[:, g, :]), in_=by_halves(bank[:]))
+
+        residual = keep.tile([P, TOKEN_TILES, D], F32)
+        bank = spread_row(PASSES)
+        for i in range(TOKEN_TILES):
+            nc.vector.tensor_tensor(
+                out=residual[:, i, :], in0=bank[:], in1=h_tok[:, i, :], op=ALU.add
+            )
+
+        ff = [
+            psum_ff.tile([P, D], F32, name="ff%d" % i, tag="ff%d" % i) for i in range(TOKEN_TILES)
+        ]
+        x_of = {}
+        a_tok_of = {}
+        aT_of = {}
+        grouped_of = {}
+        a_mx_of = {}
+
+        def passes_of(r):
+            return range(r * ROUND, (r + 1) * ROUND)
+
+        def first_product(r):
+            for g in passes_of(r):
+                plane = g // (PASSES // PLANES)
+                cols = slice((g % (PASSES // PLANES)) * K_PASS, (g % (PASSES // PLANES) + 1) * K_PASS)
+                for i in range(TOKEN_TILES):
+                    x = psum_x.tile([P, K_PASS], F32, tag="x")
+                    nc.tensor.matmul_mx(
+                        out=x[:],
+                        lhsT=h_codes[:, token_tile(i)].bitcast(FP8X4),
+                        lhsT_scale=h_scales[:, token_tile(i)],
+                        rhs=w1_words[:, g * K_PASS : (g + 1) * K_PASS].bitcast(FP8X4),
+                        rhs_scale=w1_planes[4 * plane : P, cols],
+                        start=True,
+                        stop=True,
+                    )
+                    x_of[(g, i)] = x
+
+        def add_bias(r):
+            a_tok = work.tile([P, ROUND, TOKEN_TILES, K_PASS], BF16, tag="a_tok")
+            for j, g in enumerate(passes_of(r)):
+                for i in range(TOKEN_TILES):
+                    nc.vector.tensor_tensor(
+                        out=halves_apart(a_tok[:, j, i, :]),
+                        in0=by_halves(x_of[(g, i)][:]),
+                        in1=halves_apart(bias_all[:, g, :]),
+                        op=ALU.add,
+                    )
+            a_tok_of[r] = a_tok
+
+        def transposes(r):
+            a_tok = a_tok_of[r]
+            for j, g in enumerate(passes_of(r)):
+                aT = psum_t.tile([P, HALVES, TOKENS], F32, tag="aT")
+                for i in range(TOKEN_TILES):
+                    a_halves = a_tok[:, j, i, :].bitcast(F32)
+                    for u in range(HALVES):
+                        nc.tensor.transpose(
+                            aT[:, u, token_tile(i)], a_halves[:, u * P : (u + 1) * P], ident_f32[:]
+                        )
+                aT_of[g] = aT
+
+        def relu_regroup(r):
+            grouped = work.tile([P, ROUND, TOKENS * PACK], BF16, tag="grouped", align_bytes=64)
+            for j, g in enumerate(passes_of(r)):
+                nc.scalar.activation(
+                    out=grouped[:, j, :].rearrange("p (t u e) -> p t u e", u=HALVES, e=PAIR),
+                    in_=aT_of[g][:].bitcast(BF16).rearrange("p u (t e) -> p t u e", e=PAIR),
+                    func=ACT.Relu,
+                )
+            grouped_of[r] = grouped
+
+        def quantise(r):
+            a_codes = work.tile([P, ROUND * TOKENS], U32, tag="a_codes", align_bytes=64)
+            a_scales = work.tile([P, ROUND * TOKENS], U8, tag="a_scales", align_bytes=64)
+            nc.vector.quantize_mx(
+                out=a_codes[:].bitcast(FP8X4),
+                scales=a_scales[:],
+                in_=grouped_of[r][:].rearrange("p j c -> p (j c)"),
+            )
+            a_mx_of[r] = (a_codes, a_scales)
+
+        def second_product(r):
+            a_codes, a_scales = a_mx_of[r]
+            for j, g in enumerate(passes_of(r)):
+                for i in range(TOKEN_TILES):
+                    cols = slice(j * TOKENS + i * P, j * TOKENS + (i + 1) * P)
+                    nc.tensor.matmul_mx(
+                        out=ff[i][:],
+                        lhsT=a_codes[:, cols].bitcast(FP8X4),
+                        lhsT_scale=a_scales[:, cols],
+                        rhs=w2_words[:, g, :].bitcast(FP8X4),
+                        rhs_scale=w2_planes[:, g, :],
+                        start=(g == 0),
+                        stop=(g == PASSES - 1),
+                    )
+
+        for s in range(ROUNDS + 3):
+            if s < ROUNDS:
+                first_product(s)
+                add_bias(s)
+            if 0 <= s - 1 < ROUNDS:
+                transposes(s - 1)
+                relu_regroup(s - 1)
+            if 0 <= s - 2 < ROUNDS:
+                quantise(s - 2)
+            if 0 <= s - 3 < ROUNDS:
+                second_product(s - 3)
+
+        t_all = keep.tile([P, TOKEN_TILES, D], F32)
+        row_sum = keep.tile([P, TOKEN_TILES], F32)
+        for i in range(TOKEN_TILES):
+            nc.vector.scalar_tensor_tensor(
+                out=t_all[:, i, :],
+                in0=ff[i][:],
+                scalar=1.0,
+                in1=residual[:, i, :],
+                op0=ALU.mult,
+                op1=ALU.add,
+                accum_out=row_sum[:, i : i + 1],
+            )
+        mean_bank = psum_x.tile([P, K_PASS], F32, tag="x")
+        nc.tensor.matmul(
+            out=mean_bank[:, 0:TOKEN_TILES], lhsT=neg_average[:], rhs=row_sum[:], start=True, stop=True
+        )
+        neg_mean = keep.tile([P, 1], F32)
+        nc.vector.reduce_sum(
+            out=neg_mean[:], in_=mean_bank[:, 0:TOKEN_TILES], axis=mybir.AxisListType.X
+        )
+        y = keep.tile([P, TOKEN_TILES, D], F32)
+        row_square = keep.tile([P, TOKEN_TILES], F32)
+        for i in range(TOKEN_TILES):
+            nc.scalar.activation(
+                out=y[:, i, :],
+                in_=t_all[:, i, :],
+                func=ACT.Square,
+                bias=neg_mean[:],
+                scale=1.0,
+                accum_out=row_square[:, i : i + 1],
+            )
+        var_bank = psum_x.tile([P, K_PASS], F32, tag="x")
+        nc.tensor.matmul(
+            out=var_bank[:, 0:TOKEN_TILES], lhsT=neg_average[:], rhs=row_square[:], start=True, stop=True
+        )
+        neg_var = keep.tile([P, 1], F32)
+        nc.vector.reduce_sum(
+            out=neg_var[:], in_=var_bank[:, 0:TOKEN_TILES], axis=mybir.AxisListType.X
+        )
+        std = keep.tile([P, 1], F32)
+        nc.scalar.activation(out=std[:], in_=neg_var[:], func=ACT.Sqrt, bias=eps_col[:], scale=-1.0)
+        inv_std = keep.tile([P, 1], F32)
+        nc.vector.reciprocal(out=inv_std[:], in_=std[:])
+        for i in range(TOKEN_TILES):
+            nc.vector.tensor_scalar(
+                out=y[:, i, :],
+                in0=t_all[:, i, :],
+                scalar1=neg_mean[:],
+                scalar2=inv_std[:],
+                op0=ALU.add,
+                op1=ALU.mult,
+            )
+            nc.sync.dma_start(out=out[i], in_=y[:, i, :])

@@ -23,8 +23,10 @@ D = 512
 F = 16384
 PASSES = F // K_PASS
 PLANES = 4
+PER_PLANE = PASSES // PLANES
 ROUND = 2
 ROUNDS = PASSES // ROUND
+CHUNKS = PER_PLANE // ROUND
 EPS = 1e-5
 
 FLOPS = 2 * TOKENS * D * F * 2
@@ -36,14 +38,33 @@ def tile_decoderblock_pb_k_kernel(
     nc = tc.nc
     with ExitStack() as ctx:
         keep = ctx.enter_context(tc.tile_pool(name="keep", bufs=1))
-        work = ctx.enter_context(tc.tile_pool(name="work", bufs=2))
+        work = ctx.enter_context(tc.tile_pool(name="work", bufs=4))
         psum_ff = ctx.enter_context(tc.psum_pool(name="psum_ff", bufs=1))
-        psum_x = ctx.enter_context(tc.psum_pool(name="psum_x", bufs=ROUND * TOKEN_TILES))
-        psum_t = ctx.enter_context(tc.psum_pool(name="psum_t", bufs=ROUND))
+        psum_x = ctx.enter_context(tc.psum_pool(name="psum_x", bufs=6))
         ctx.enter_context(tc.manual_schedule())
+
+        def first_pass_of(r):
+            return PER_PLANE * (r % PLANES) + ROUND * (r // PLANES)
+
+        order = [first_pass_of(r) + j for r in range(ROUNDS) for j in range(ROUND)]
 
         h_tok = keep.tile([P, TOKEN_TILES, D], BF16)
         nc.sync.dma_start(out=h_tok[:], in_=h2.rearrange("i p d -> p i d"))
+
+        w1_words = keep.tile([P, F], U32, align_bytes=64)
+        w2_words = keep.tile([P, PASSES, D], U32, align_bytes=64)
+        w1_dram = w_ff1_words[0].rearrange("p n t -> p (n t)").bitcast(I32)
+        w2_dram = w_ff2_words.rearrange("g p n t -> p g (n t)").bitcast(I32)
+
+        def load_w1(g, count):
+            cols = slice(g * K_PASS, (g + count) * K_PASS)
+            nc.sync.dma_start(out=w1_words[:, cols].bitcast(I32), in_=w1_dram[:, cols])
+
+        def load_w2(g, count):
+            some = slice(g, g + count)
+            nc.sync.dma_start(out=w2_words[:, some, :].bitcast(I32), in_=w2_dram[:, some, :])
+
+        load_w1(order[0], 1)
 
         bias_rows = keep.tile([P, K_PASS], BF16)
         nc.vector.memset(bias_rows[:], 0.0)
@@ -63,52 +84,44 @@ def tile_decoderblock_pb_k_kernel(
                 .rearrange("r (j c) -> j r c", j=PLANES)
                 .bitcast(I32),
             )
+        load_w1(order[1], 1)
+        load_w1(first_pass_of(1), ROUND)
 
-        w2_planes = keep.tile([P, PASSES, D], U8, align_bytes=64)
-        nc.vector.memset(w2_planes[:].rearrange("p g n -> p (g n)").bitcast(I32), 0)
-
-        w1_words = keep.tile([P, F], U32, align_bytes=64)
-        w2_words = keep.tile([P, PASSES, D], U32, align_bytes=64)
-        w1_dram = w_ff1_words[0].rearrange("p n t -> p (n t)").bitcast(I32)
-        w2_dram = w_ff2_words.rearrange("g p n t -> p g (n t)").bitcast(I32)
-
-        def load_w1(r):
-            cols = slice(r * ROUND * K_PASS, (r + 1) * ROUND * K_PASS)
-            nc.sync.dma_start(out=w1_words[:, cols].bitcast(I32), in_=w1_dram[:, cols])
-
-        def load_w2(r):
-            some = slice(r * ROUND, (r + 1) * ROUND)
-            nc.sync.dma_start(out=w2_words[:, some, :].bitcast(I32), in_=w2_dram[:, some, :])
-
-        load_w1(0)
-        load_w1(1)
+        w2_planes = keep.tile([P, PER_PLANE, D], U8, align_bytes=64)
+        nc.vector.memset(w2_planes[:].rearrange("p c n -> p (c n)").bitcast(I32), 0)
         for quadrant in range(4):
-            nc.sync.dma_start(
-                out=w2_planes[32 * quadrant : 32 * quadrant + 4, :, :].bitcast(I32),
-                in_=w_ff2_scales[:, 4 * quadrant : 4 * quadrant + 4, :]
-                .rearrange("g r n -> r g n")
-                .bitcast(I32),
-            )
+            for plane in range(PLANES):
+                row = 32 * quadrant + 4 * plane
+                nc.sync.dma_start(
+                    out=w2_planes[row : row + 4, :, :].bitcast(I32),
+                    in_=w_ff2_scales[
+                        plane * PER_PLANE : (plane + 1) * PER_PLANE,
+                        4 * quadrant : 4 * quadrant + 4,
+                        :,
+                    ]
+                    .rearrange("c r n -> r c n")
+                    .bitcast(I32),
+                )
         for r in range(ROUNDS):
-            load_w2(r)
+            load_w2(first_pass_of(r), ROUND)
             if r + 2 < ROUNDS:
-                load_w1(r + 2)
+                load_w1(first_pass_of(r + 2), ROUND)
 
         ident_f32 = keep.tile([P, P], F32)
         make_identity(nc, ident_f32[:])
         ident_bf16 = keep.tile([P, P], BF16)
         make_identity(nc, ident_bf16[:])
         neg_average = keep.tile([P, P], F32)
-        nc.vector.memset(neg_average[:], -1.0 / (TOKENS * D))
+        nc.gpsimd.memset(neg_average[:], -1.0 / (TOKENS * D))
         eps_col = keep.tile([P, 1], F32)
-        nc.vector.memset(eps_col[:], EPS)
+        nc.gpsimd.memset(eps_col[:], EPS)
         warm_sqrt = keep.tile([P, 1], F32)
         nc.scalar.activation(out=warm_sqrt[:], in_=eps_col[:], func=ACT.Sqrt)
 
         def token_tile(i):
             return slice(i * P, (i + 1) * P)
 
-        hT = psum_t.tile([P, HALVES, TOKENS], F32, tag="aT")
+        hT = psum_x.tile([P, HALVES, TOKENS], F32, tag="x")
         for i in range(TOKEN_TILES):
             h_halves = h_tok[:, i, :].bitcast(F32)
             for u in range(HALVES):
@@ -126,136 +139,148 @@ def tile_decoderblock_pb_k_kernel(
             out=h_codes[:].bitcast(FP8X4), scales=h_scales[:], in_=h_grouped[:]
         )
 
-        def spread_row(row):
-            bank = psum_x.tile([P, K_PASS], F32, tag="x")
-            nc.tensor.matmul(
-                out=bank[:],
-                lhsT=ident_bf16[:, row : row + 1].to_broadcast([P, P]),
-                rhs=bias_rows[:],
-                start=True,
-                stop=True,
+        biasT = psum_x.tile([P, HALVES, P], F32, tag="x")
+        bias_halves = bias_rows[:].bitcast(F32)
+        for u in range(HALVES):
+            nc.tensor.transpose(
+                biasT[:, u, :], bias_halves[:, u : K_PASS // PAIR : HALVES], ident_f32[:]
             )
-            return bank
-
-        def by_halves(ap):
-            return ap.rearrange("q (p u e) -> q u p e", u=HALVES, e=PAIR)
-
-        def halves_apart(ap):
-            return ap.rearrange("q (u p e) -> q u p e", u=HALVES, e=PAIR)
-
-        bias_all = keep.tile([P, PASSES, K_PASS], BF16)
-        for g in range(PASSES):
-            bank = spread_row(g)
-            if g % 2 == 0:
-                nc.vector.tensor_copy(out=halves_apart(bias_all[:, g, :]), in_=by_halves(bank[:]))
-            else:
-                nc.scalar.copy(out=halves_apart(bias_all[:, g, :]), in_=by_halves(bank[:]))
+        bias_col = keep.tile([P, PASSES, PACK], F32)
+        nc.scalar.copy(
+            out=bias_col[:].rearrange("p g (u e) -> p u g e", u=HALVES),
+            in_=biasT[:].bitcast(BF16).rearrange("p u (g e) -> p u g e", e=PAIR)[:, :, 0:PASSES, :],
+        )
 
         residual = keep.tile([P, TOKEN_TILES, D], F32)
-        bank = spread_row(PASSES)
-        for i in range(TOKEN_TILES):
-            nc.vector.tensor_tensor(
-                out=residual[:, i, :], in0=bank[:], in1=h_tok[:, i, :], op=ALU.add
-            )
+        bank = psum_x.tile([P, K_PASS], F32, tag="x")
+        nc.tensor.matmul(
+            out=bank[:],
+            lhsT=ident_bf16[:, PASSES : PASSES + 1].to_broadcast([P, P]),
+            rhs=bias_rows[:],
+            start=True,
+            stop=True,
+        )
+
+        def add_residual():
+            for i in range(TOKEN_TILES):
+                nc.vector.tensor_tensor(
+                    out=residual[:, i, :], in0=bank[:], in1=h_tok[:, i, :], op=ALU.add
+                )
 
         ff = [
             psum_ff.tile([P, D], F32, name="ff%d" % i, tag="ff%d" % i) for i in range(TOKEN_TILES)
         ]
+        w1_scales_of = {}
+        w1_codes_of = {}
         x_of = {}
-        a_tok_of = {}
-        aT_of = {}
+        a_of = {}
         grouped_of = {}
         a_mx_of = {}
 
-        def passes_of(r):
-            return range(r * ROUND, (r + 1) * ROUND)
+        def permute_scales(chunk):
+            scales = keep.tile(
+                [P, ROUND * K_PASS], U8, align_bytes=64, name="w1_scales%d" % chunk
+            )
+            nc.vector.tensor_copy(
+                out=scales[:].rearrange("p (c t m) -> p c m t", t=PACK, m=P),
+                in_=w1_planes[:, chunk * ROUND * K_PASS : (chunk + 1) * ROUND * K_PASS].rearrange(
+                    "p (c m t) -> p c m t", t=PACK, m=P
+                ),
+            )
+            w1_scales_of[chunk] = scales
 
-        def first_product(r):
-            for g in passes_of(r):
-                plane = g // (PASSES // PLANES)
-                cols = slice((g % (PASSES // PLANES)) * K_PASS, (g % (PASSES // PLANES) + 1) * K_PASS)
-                for i in range(TOKEN_TILES):
-                    x = psum_x.tile([P, K_PASS], F32, tag="x")
+        def permute_words(s):
+            g = order[s]
+            codes = work.tile([P, K_PASS], U32, tag="w1_codes", align_bytes=64)
+            nc.vector.tensor_copy(
+                out=codes[:].bitcast(I32).rearrange("p (t c i) -> p c t i", t=PACK, i=4),
+                in_=w1_words[:, g * K_PASS : (g + 1) * K_PASS]
+                .bitcast(I32)
+                .rearrange("p (c i t) -> p c t i", t=PACK, i=4),
+            )
+            w1_codes_of[s] = codes
+
+        def first_product(s):
+            g = order[s]
+            plane = g // PER_PLANE
+            scales = w1_scales_of[s // (PLANES * ROUND)]
+            for half in range(2):
+                x = psum_x.tile([P, 2, TOKENS], F32, tag="x")
+                for j in range(2):
+                    t = 2 * half + j
+                    col = (g % ROUND) * K_PASS + t * P
                     nc.tensor.matmul_mx(
-                        out=x[:],
-                        lhsT=h_codes[:, token_tile(i)].bitcast(FP8X4),
-                        lhsT_scale=h_scales[:, token_tile(i)],
-                        rhs=w1_words[:, g * K_PASS : (g + 1) * K_PASS].bitcast(FP8X4),
-                        rhs_scale=w1_planes[4 * plane : P, cols],
+                        out=x[:, j, :],
+                        lhsT=w1_codes_of[s][:, t * P : (t + 1) * P].bitcast(FP8X4),
+                        lhsT_scale=scales[4 * plane : P, col : col + P],
+                        rhs=h_codes[:].bitcast(FP8X4),
+                        rhs_scale=h_scales[:],
                         start=True,
                         stop=True,
                     )
-                    x_of[(g, i)] = x
+                x_of[(s, half)] = x
 
-        def add_bias(r):
-            a_tok = work.tile([P, ROUND, TOKEN_TILES, K_PASS], BF16, tag="a_tok")
-            for j, g in enumerate(passes_of(r)):
-                for i in range(TOKEN_TILES):
-                    nc.vector.tensor_tensor(
-                        out=halves_apart(a_tok[:, j, i, :]),
-                        in0=by_halves(x_of[(g, i)][:]),
-                        in1=halves_apart(bias_all[:, g, :]),
-                        op=ALU.add,
-                    )
-            a_tok_of[r] = a_tok
-
-        def transposes(r):
-            a_tok = a_tok_of[r]
-            for j, g in enumerate(passes_of(r)):
-                aT = psum_t.tile([P, HALVES, TOKENS], F32, tag="aT")
-                for i in range(TOKEN_TILES):
-                    a_halves = a_tok[:, j, i, :].bitcast(F32)
-                    for u in range(HALVES):
-                        nc.tensor.transpose(
-                            aT[:, u, token_tile(i)], a_halves[:, u * P : (u + 1) * P], ident_f32[:]
-                        )
-                aT_of[g] = aT
-
-        def relu_regroup(r):
-            grouped = work.tile([P, ROUND, TOKENS * PACK], BF16, tag="grouped", align_bytes=64)
-            for j, g in enumerate(passes_of(r)):
+        def bias_relu(s):
+            g = order[s]
+            a = work.tile([P, PACK, TOKENS], BF16, tag="a")
+            for t in range(PACK):
                 nc.scalar.activation(
-                    out=grouped[:, j, :].rearrange("p (t u e) -> p t u e", u=HALVES, e=PAIR),
-                    in_=aT_of[g][:].bitcast(BF16).rearrange("p u (t e) -> p t u e", e=PAIR),
+                    out=a[:, t, :],
+                    in_=x_of[(s, t // 2)][:, t % 2, :],
                     func=ACT.Relu,
+                    bias=bias_col[:, g, t : t + 1],
+                    scale=1.0,
                 )
-            grouped_of[r] = grouped
+            a_of[s] = a
 
-        def quantise(r):
-            a_codes = work.tile([P, ROUND * TOKENS], U32, tag="a_codes", align_bytes=64)
-            a_scales = work.tile([P, ROUND * TOKENS], U8, tag="a_scales", align_bytes=64)
-            nc.vector.quantize_mx(
-                out=a_codes[:].bitcast(FP8X4),
-                scales=a_scales[:],
-                in_=grouped_of[r][:].rearrange("p j c -> p (j c)"),
+        def interleave(s):
+            grouped = work.tile([P, TOKENS * PACK], BF16, tag="grouped", align_bytes=64)
+            nc.vector.tensor_copy(
+                out=grouped[:].rearrange("p (c i t) -> p c t i", t=PACK, i=4),
+                in_=a_of[s][:].rearrange("p t (c i) -> p c t i", i=4),
             )
-            a_mx_of[r] = (a_codes, a_scales)
+            grouped_of[s] = grouped
 
-        def second_product(r):
-            a_codes, a_scales = a_mx_of[r]
-            for j, g in enumerate(passes_of(r)):
-                for i in range(TOKEN_TILES):
-                    cols = slice(j * TOKENS + i * P, j * TOKENS + (i + 1) * P)
-                    nc.tensor.matmul_mx(
-                        out=ff[i][:],
-                        lhsT=a_codes[:, cols].bitcast(FP8X4),
-                        lhsT_scale=a_scales[:, cols],
-                        rhs=w2_words[:, g, :].bitcast(FP8X4),
-                        rhs_scale=w2_planes[:, g, :],
-                        start=(g == 0),
-                        stop=(g == PASSES - 1),
-                    )
+        def quantise(s):
+            a_codes = work.tile([P, TOKENS], U32, tag="a_codes", align_bytes=64)
+            a_scales = work.tile([P, TOKENS], U8, tag="a_scales", align_bytes=64)
+            nc.vector.quantize_mx(
+                out=a_codes[:].bitcast(FP8X4), scales=a_scales[:], in_=grouped_of[s][:]
+            )
+            a_mx_of[s] = (a_codes, a_scales)
 
-        for s in range(ROUNDS + 3):
-            if s < ROUNDS:
+        def second_product(s):
+            g = order[s]
+            plane = g // PER_PLANE
+            a_codes, a_scales = a_mx_of[s]
+            for i in range(TOKEN_TILES):
+                nc.tensor.matmul_mx(
+                    out=ff[i][:],
+                    lhsT=a_codes[:, token_tile(i)].bitcast(FP8X4),
+                    lhsT_scale=a_scales[:, token_tile(i)],
+                    rhs=w2_words[:, g, :].bitcast(FP8X4),
+                    rhs_scale=w2_planes[4 * plane : P, g % PER_PLANE, :],
+                    start=(s == 0),
+                    stop=(s == PASSES - 1),
+                )
+
+        permute_words(0)
+        permute_scales(0)
+        permute_words(1)
+        add_residual()
+        for s in range(PASSES + 3):
+            if s < PASSES:
                 first_product(s)
-                add_bias(s)
-            if 0 <= s - 1 < ROUNDS:
-                transposes(s - 1)
-                relu_regroup(s - 1)
-            if 0 <= s - 2 < ROUNDS:
+                bias_relu(s)
+            if s + 2 < PASSES:
+                permute_words(s + 2)
+            if (s + 4) % (PLANES * ROUND) == 0 and (s + 4) // (PLANES * ROUND) < CHUNKS:
+                permute_scales((s + 4) // (PLANES * ROUND))
+            if 0 <= s - 1 < PASSES:
+                interleave(s - 1)
+            if 0 <= s - 2 < PASSES:
                 quantise(s - 2)
-            if 0 <= s - 3 < ROUNDS:
+            if 0 <= s - 3 < PASSES:
                 second_product(s - 3)
 
         t_all = keep.tile([P, TOKEN_TILES, D], F32)

@@ -38,7 +38,7 @@ def tile_decoderblock_pb_k_kernel(
     nc = tc.nc
     with ExitStack() as ctx:
         keep = ctx.enter_context(tc.tile_pool(name="keep", bufs=1))
-        work = ctx.enter_context(tc.tile_pool(name="work", bufs=4))
+        work = ctx.enter_context(tc.tile_pool(name="work", bufs=5))
         psum_ff = ctx.enter_context(tc.psum_pool(name="psum_ff", bufs=1))
         psum_x = ctx.enter_context(tc.psum_pool(name="psum_x", bufs=6))
         ctx.enter_context(tc.manual_schedule())
@@ -47,6 +47,9 @@ def tile_decoderblock_pb_k_kernel(
             return PER_PLANE * (r % PLANES) + ROUND * (r // PLANES)
 
         order = [first_pass_of(r) + j for r in range(ROUNDS) for j in range(ROUND)]
+
+        eps_col = keep.tile([P, 1], F32)
+        nc.vector.memset(eps_col[:], EPS)
 
         h_tok = keep.tile([P, TOKEN_TILES, D], BF16)
         nc.sync.dma_start(out=h_tok[:], in_=h2.rearrange("i p d -> p i d"))
@@ -64,6 +67,23 @@ def tile_decoderblock_pb_k_kernel(
             some = slice(g, g + count)
             nc.sync.dma_start(out=w2_words[:, some, :].bitcast(I32), in_=w2_dram[:, some, :])
 
+        chunk_cols = ROUND * K_PASS
+        rest_cols = (CHUNKS - 1) * chunk_cols
+        w1_planes_first = keep.tile([P, chunk_cols], U8, align_bytes=64)
+        nc.vector.memset(w1_planes_first[:].bitcast(I32), 0)
+        w1_planes_rest = keep.tile([P, rest_cols], U8, align_bytes=64)
+        nc.vector.memset(w1_planes_rest[:].bitcast(I32), 0)
+
+        def load_w1_scales(planes, cols):
+            for quadrant in range(4):
+                nc.sync.dma_start(
+                    out=planes[32 * quadrant : 32 * quadrant + 4 * PLANES, :].bitcast(I32),
+                    in_=w_ff1_scales[0, 4 * quadrant : 4 * quadrant + 4, :]
+                    .rearrange("r (j c) -> j r c", j=PLANES)[:, :, cols]
+                    .bitcast(I32),
+                )
+
+        load_w1_scales(w1_planes_first, slice(0, chunk_cols))
         load_w1(order[0], 1)
 
         bias_rows = keep.tile([P, K_PASS], BF16)
@@ -75,22 +95,20 @@ def tile_decoderblock_pb_k_kernel(
             out=bias_rows[PASSES : PASSES + 1, :], in_=b_ff2.rearrange("(o c) -> o c", o=1)
         )
 
-        w1_planes = keep.tile([P, F // PLANES], U8, align_bytes=64)
-        nc.vector.memset(w1_planes[:].bitcast(I32), 0)
-        for quadrant in range(4):
-            nc.sync.dma_start(
-                out=w1_planes[32 * quadrant : 32 * quadrant + 4 * PLANES, :].bitcast(I32),
-                in_=w_ff1_scales[0, 4 * quadrant : 4 * quadrant + 4, :]
-                .rearrange("r (j c) -> j r c", j=PLANES)
-                .bitcast(I32),
-            )
         load_w1(order[1], 1)
+        load_w1_scales(w1_planes_rest, slice(chunk_cols, CHUNKS * chunk_cols))
         load_w1(first_pass_of(1), ROUND)
+        load_w1(first_pass_of(2), ROUND)
 
+        ident_f32 = keep.tile([P, P], F32)
+        make_identity(nc, ident_f32[:])
+        ident_bf16 = keep.tile([P, P], BF16)
+        make_identity(nc, ident_bf16[:])
         w2_planes = keep.tile([P, PER_PLANE, D], U8, align_bytes=64)
-        nc.vector.memset(w2_planes[:].rearrange("p c n -> p (c n)").bitcast(I32), 0)
-        for quadrant in range(4):
-            for plane in range(PLANES):
+        nc.gpsimd.memset(w2_planes[:].rearrange("p c n -> p (c n)").bitcast(I32), 0)
+
+        def load_w2_scales(plane):
+            for quadrant in range(4):
                 row = 32 * quadrant + 4 * plane
                 nc.sync.dma_start(
                     out=w2_planes[row : row + 4, :, :].bitcast(I32),
@@ -102,21 +120,18 @@ def tile_decoderblock_pb_k_kernel(
                     .rearrange("c r n -> r c n")
                     .bitcast(I32),
                 )
-        for r in range(ROUNDS):
-            load_w2(first_pass_of(r), ROUND)
-            if r + 2 < ROUNDS:
-                load_w1(first_pass_of(r + 2), ROUND)
 
-        ident_f32 = keep.tile([P, P], F32)
-        make_identity(nc, ident_f32[:])
-        ident_bf16 = keep.tile([P, P], BF16)
-        make_identity(nc, ident_bf16[:])
+        for r in range(ROUNDS):
+            if r < PLANES:
+                load_w2_scales(r)
+            load_w2(first_pass_of(r), ROUND)
+            if r + 3 < ROUNDS:
+                load_w1(first_pass_of(r + 3), ROUND)
+
         neg_average = keep.tile([P, P], F32)
         nc.gpsimd.memset(neg_average[:], -1.0 / (TOKENS * D))
-        eps_col = keep.tile([P, 1], F32)
-        nc.gpsimd.memset(eps_col[:], EPS)
-        warm_sqrt = keep.tile([P, 1], F32)
-        nc.scalar.activation(out=warm_sqrt[:], in_=eps_col[:], func=ACT.Sqrt)
+        warm = keep.tile([P, 1], F32)
+        nc.scalar.activation(out=warm[:], in_=eps_col[:], func=ACT.Abs_reciprocal_sqrt)
 
         def token_tile(i):
             return slice(i * P, (i + 1) * P)
@@ -129,15 +144,12 @@ def tile_decoderblock_pb_k_kernel(
                     hT[:, u, token_tile(i)], h_halves[:, u : D // PAIR : HALVES], ident_f32[:]
                 )
         h_grouped = keep.tile([P, TOKENS * PACK], BF16, align_bytes=64)
-        nc.vector.tensor_copy(
+        nc.scalar.copy(
             out=h_grouped[:].bitcast(F32).rearrange("p (t u) -> p t u", u=HALVES),
             in_=hT[:].rearrange("p u t -> p t u"),
         )
         h_codes = keep.tile([P, TOKENS], U32, align_bytes=64)
         h_scales = keep.tile([P, TOKENS], U8, align_bytes=64)
-        nc.vector.quantize_mx(
-            out=h_codes[:].bitcast(FP8X4), scales=h_scales[:], in_=h_grouped[:]
-        )
 
         biasT = psum_x.tile([P, HALVES, P], F32, tag="x")
         bias_halves = bias_rows[:].bitcast(F32)
@@ -152,20 +164,45 @@ def tile_decoderblock_pb_k_kernel(
         )
 
         residual = keep.tile([P, TOKEN_TILES, D], F32)
-        bank = psum_x.tile([P, K_PASS], F32, tag="x")
-        nc.tensor.matmul(
-            out=bank[:],
-            lhsT=ident_bf16[:, PASSES : PASSES + 1].to_broadcast([P, P]),
-            rhs=bias_rows[:],
-            start=True,
-            stop=True,
-        )
+        residual_sum = keep.tile([P, TOKEN_TILES], F32)
 
-        def add_residual():
-            for i in range(TOKEN_TILES):
-                nc.vector.tensor_tensor(
-                    out=residual[:, i, :], in0=bank[:], in1=h_tok[:, i, :], op=ALU.add
+        def add_residual(i):
+            bank = psum_x.tile([P, D], F32, tag="x")
+            nc.tensor.matmul(
+                out=bank[:], lhsT=ident_bf16[:], rhs=h_tok[:, i, :], start=True, stop=False
+            )
+            nc.tensor.matmul(
+                out=bank[:],
+                lhsT=ident_bf16[:, PASSES : PASSES + 1].to_broadcast([P, P]),
+                rhs=bias_rows[:],
+                start=False,
+                stop=True,
+            )
+            nc.scalar.activation(
+                out=residual[:, i, :],
+                in_=bank[:],
+                func=ACT.Identity,
+                accum_out=residual_sum[:, i : i + 1],
+            )
+
+        def minus_average(columns):
+            width = columns[0].shape[1]
+            bank = psum_x.tile([P, K_PASS], F32, tag="x")
+            for j, column in enumerate(columns):
+                nc.tensor.matmul(
+                    out=bank[:, 0:width],
+                    lhsT=neg_average[:],
+                    rhs=column,
+                    start=(j == 0),
+                    stop=(j == len(columns) - 1),
                 )
+            return bank[:, 0:width]
+
+        neg_pivot = keep.tile([P, 1], F32)
+
+        def make_pivot():
+            minus_c = minus_average([residual_sum[:, i : i + 1] for i in range(TOKEN_TILES)])
+            nc.scalar.copy(out=neg_pivot[:], in_=minus_c)
 
         ff = [
             psum_ff.tile([P, D], F32, name="ff%d" % i, tag="ff%d" % i) for i in range(TOKEN_TILES)
@@ -178,14 +215,16 @@ def tile_decoderblock_pb_k_kernel(
         a_mx_of = {}
 
         def permute_scales(chunk):
+            if chunk == 0:
+                raw = w1_planes_first[:]
+            else:
+                raw = w1_planes_rest[:, (chunk - 1) * chunk_cols : chunk * chunk_cols]
             scales = keep.tile(
-                [P, ROUND * K_PASS], U8, align_bytes=64, name="w1_scales%d" % chunk
+                [P, chunk_cols], U8, align_bytes=64, name="w1_scales%d" % chunk
             )
             nc.vector.tensor_copy(
                 out=scales[:].rearrange("p (c t m) -> p c m t", t=PACK, m=P),
-                in_=w1_planes[:, chunk * ROUND * K_PASS : (chunk + 1) * ROUND * K_PASS].rearrange(
-                    "p (c m t) -> p c m t", t=PACK, m=P
-                ),
+                in_=raw.rearrange("p (c m t) -> p c m t", t=PACK, m=P),
             )
             w1_scales_of[chunk] = scales
 
@@ -264,14 +303,20 @@ def tile_decoderblock_pb_k_kernel(
                     stop=(s == PASSES - 1),
                 )
 
-        permute_words(0)
         permute_scales(0)
+        permute_words(0)
+        nc.vector.quantize_mx(
+            out=h_codes[:].bitcast(FP8X4), scales=h_scales[:], in_=h_grouped[:]
+        )
         permute_words(1)
-        add_residual()
-        for s in range(PASSES + 3):
+        for s in range(PASSES + 4):
             if s < PASSES:
                 first_product(s)
                 bias_relu(s)
+            if s in (2, 3):
+                add_residual(s - 2)
+            if s == 4:
+                make_pivot()
             if s + 2 < PASSES:
                 permute_words(s + 2)
             if (s + 4) % (PLANES * ROUND) == 0 and (s + 4) // (PLANES * ROUND) < CHUNKS:
@@ -280,11 +325,12 @@ def tile_decoderblock_pb_k_kernel(
                 interleave(s - 1)
             if 0 <= s - 2 < PASSES:
                 quantise(s - 2)
-            if 0 <= s - 3 < PASSES:
-                second_product(s - 3)
+            if 0 <= s - 4 < PASSES:
+                second_product(s - 4)
 
         t_all = keep.tile([P, TOKEN_TILES, D], F32)
-        row_sum = keep.tile([P, TOKEN_TILES], F32)
+        square = keep.tile([P, TOKEN_TILES, D], F32)
+        sums = keep.tile([P, TOKEN_TILES, 2], F32)
         for i in range(TOKEN_TILES):
             nc.vector.scalar_tensor_tensor(
                 out=t_all[:, i, :],
@@ -293,39 +339,37 @@ def tile_decoderblock_pb_k_kernel(
                 in1=residual[:, i, :],
                 op0=ALU.mult,
                 op1=ALU.add,
-                accum_out=row_sum[:, i : i + 1],
+                accum_out=sums[:, i, 0:1],
             )
-        mean_bank = psum_x.tile([P, K_PASS], F32, tag="x")
-        nc.tensor.matmul(
-            out=mean_bank[:, 0:TOKEN_TILES], lhsT=neg_average[:], rhs=row_sum[:], start=True, stop=True
-        )
-        neg_mean = keep.tile([P, 1], F32)
-        nc.vector.reduce_sum(
-            out=neg_mean[:], in_=mean_bank[:, 0:TOKEN_TILES], axis=mybir.AxisListType.X
-        )
-        y = keep.tile([P, TOKEN_TILES, D], F32)
-        row_square = keep.tile([P, TOKEN_TILES], F32)
-        for i in range(TOKEN_TILES):
             nc.scalar.activation(
-                out=y[:, i, :],
+                out=square[:, i, :],
                 in_=t_all[:, i, :],
                 func=ACT.Square,
-                bias=neg_mean[:],
+                bias=neg_pivot[:],
                 scale=1.0,
-                accum_out=row_square[:, i : i + 1],
+                accum_out=sums[:, i, 1:2],
             )
-        var_bank = psum_x.tile([P, K_PASS], F32, tag="x")
-        nc.tensor.matmul(
-            out=var_bank[:, 0:TOKEN_TILES], lhsT=neg_average[:], rhs=row_square[:], start=True, stop=True
+        moments = minus_average([sums[:, i, :] for i in range(TOKEN_TILES)])
+        shift = keep.tile([P, 1], F32)
+        nc.vector.tensor_tensor(
+            out=shift[:], in0=moments[:, 0:1], in1=neg_pivot[:], op=ALU.subtract
         )
         neg_var = keep.tile([P, 1], F32)
-        nc.vector.reduce_sum(
-            out=neg_var[:], in_=var_bank[:, 0:TOKEN_TILES], axis=mybir.AxisListType.X
+        nc.vector.scalar_tensor_tensor(
+            out=neg_var[:],
+            in0=shift[:],
+            scalar=shift[:],
+            in1=moments[:, 1:2],
+            op0=ALU.mult,
+            op1=ALU.add,
         )
-        std = keep.tile([P, 1], F32)
-        nc.scalar.activation(out=std[:], in_=neg_var[:], func=ACT.Sqrt, bias=eps_col[:], scale=-1.0)
+        neg_mean = keep.tile([P, 1], F32)
+        nc.vector.tensor_copy(out=neg_mean[:], in_=moments[:, 0:1])
         inv_std = keep.tile([P, 1], F32)
-        nc.vector.reciprocal(out=inv_std[:], in_=std[:])
+        nc.scalar.activation(
+            out=inv_std[:], in_=neg_var[:], func=ACT.Abs_reciprocal_sqrt, bias=eps_col[:], scale=-1.0
+        )
+        y = keep.tile([P, TOKEN_TILES, D], F32)
         for i in range(TOKEN_TILES):
             nc.vector.tensor_scalar(
                 out=y[:, i, :],

@@ -38,7 +38,7 @@ def tile_decoderblock_pb_k_kernel(
     nc = tc.nc
     with ExitStack() as ctx:
         keep = ctx.enter_context(tc.tile_pool(name="keep", bufs=1))
-        work = ctx.enter_context(tc.tile_pool(name="work", bufs=5))
+        work = ctx.enter_context(tc.tile_pool(name="work", bufs=6))
         psum_ff = ctx.enter_context(tc.psum_pool(name="psum_ff", bufs=1))
         psum_x = ctx.enter_context(tc.psum_pool(name="psum_x", bufs=6))
         ctx.enter_context(tc.manual_schedule())
@@ -53,6 +53,12 @@ def tile_decoderblock_pb_k_kernel(
 
         h_tok = keep.tile([P, TOKEN_TILES, D], BF16)
         nc.sync.dma_start(out=h_tok[:], in_=h2.rearrange("i p d -> p i d"))
+
+        bias_rows = keep.tile([P, K_PASS], BF16)
+        nc.vector.memset(bias_rows[:], 0.0)
+        nc.sync.dma_start(
+            out=bias_rows[0:PASSES, :], in_=b_ff1.rearrange("(g c) -> g c", c=K_PASS)
+        )
 
         w1_words = keep.tile([P, F], U32, align_bytes=64)
         w2_words = keep.tile([P, PASSES, D], U32, align_bytes=64)
@@ -86,17 +92,7 @@ def tile_decoderblock_pb_k_kernel(
         load_w1_scales(w1_planes_first, slice(0, chunk_cols))
         load_w1(order[0], 1)
 
-        bias_rows = keep.tile([P, K_PASS], BF16)
-        nc.vector.memset(bias_rows[:], 0.0)
-        nc.sync.dma_start(
-            out=bias_rows[0:PASSES, :], in_=b_ff1.rearrange("(g c) -> g c", c=K_PASS)
-        )
-        nc.sync.dma_start(
-            out=bias_rows[PASSES : PASSES + 1, :], in_=b_ff2.rearrange("(o c) -> o c", o=1)
-        )
-
         load_w1(order[1], 1)
-        load_w1_scales(w1_planes_rest, slice(chunk_cols, CHUNKS * chunk_cols))
         load_w1(first_pass_of(1), ROUND)
         load_w1(first_pass_of(2), ROUND)
 
@@ -104,29 +100,40 @@ def tile_decoderblock_pb_k_kernel(
         make_identity(nc, ident_f32[:])
         ident_bf16 = keep.tile([P, P], BF16)
         make_identity(nc, ident_bf16[:])
-        w2_planes = keep.tile([P, PER_PLANE, D], U8, align_bytes=64)
-        nc.gpsimd.memset(w2_planes[:].rearrange("p c n -> p (c n)").bitcast(I32), 0)
+        b2_rows = keep.tile([P, D], BF16)
+        nc.gpsimd.memset(b2_rows[:], 0.0)
+        nc.gpsimd.dma_start(out=b2_rows[0:1, :], in_=b_ff2.rearrange("(o c) -> o c", o=1))
+        w2_planes = []
+        for chunk in range(CHUNKS):
+            planes = keep.tile(
+                [P, ROUND, D], U8, align_bytes=64, name="w2_planes%d" % chunk
+            )
+            nc.gpsimd.memset(planes[:].rearrange("p c n -> p (c n)").bitcast(I32), 0)
+            w2_planes.append(planes)
 
-        def load_w2_scales(plane):
-            for quadrant in range(4):
-                row = 32 * quadrant + 4 * plane
-                nc.sync.dma_start(
-                    out=w2_planes[row : row + 4, :, :].bitcast(I32),
-                    in_=w_ff2_scales[
-                        plane * PER_PLANE : (plane + 1) * PER_PLANE,
-                        4 * quadrant : 4 * quadrant + 4,
-                        :,
-                    ]
-                    .rearrange("c r n -> r c n")
-                    .bitcast(I32),
-                )
+        def load_w2_scales(chunk):
+            for c in range(ROUND):
+                for quadrant in range(4):
+                    nc.sync.dma_start(
+                        out=w2_planes[chunk][
+                            32 * quadrant : 32 * quadrant + 4 * PLANES, c, :
+                        ].bitcast(I32),
+                        in_=w_ff2_scales[
+                            chunk * ROUND + c : PASSES : PER_PLANE,
+                            4 * quadrant : 4 * quadrant + 4,
+                            :,
+                        ].bitcast(I32),
+                    )
 
+        load_w2_scales(0)
         for r in range(ROUNDS):
-            if r < PLANES:
-                load_w2_scales(r)
             load_w2(first_pass_of(r), ROUND)
             if r + 3 < ROUNDS:
                 load_w1(first_pass_of(r + 3), ROUND)
+            if r == 0:
+                load_w1_scales(w1_planes_rest, slice(chunk_cols, CHUNKS * chunk_cols))
+            if r % PLANES == 1 and r // PLANES + 1 < CHUNKS:
+                load_w2_scales(r // PLANES + 1)
 
         neg_average = keep.tile([P, P], F32)
         nc.gpsimd.memset(neg_average[:], -1.0 / (TOKENS * D))
@@ -173,8 +180,8 @@ def tile_decoderblock_pb_k_kernel(
             )
             nc.tensor.matmul(
                 out=bank[:],
-                lhsT=ident_bf16[:, PASSES : PASSES + 1].to_broadcast([P, P]),
-                rhs=bias_rows[:],
+                lhsT=ident_bf16[:, 0:1].to_broadcast([P, P]),
+                rhs=b2_rows[:],
                 start=False,
                 stop=True,
             )
@@ -298,7 +305,7 @@ def tile_decoderblock_pb_k_kernel(
                     lhsT=a_codes[:, token_tile(i)].bitcast(FP8X4),
                     lhsT_scale=a_scales[:, token_tile(i)],
                     rhs=w2_words[:, g, :].bitcast(FP8X4),
-                    rhs_scale=w2_planes[4 * plane : P, g % PER_PLANE, :],
+                    rhs_scale=w2_planes[s // (PLANES * ROUND)][4 * plane : P, g % ROUND, :],
                     start=(s == 0),
                     stop=(s == PASSES - 1),
                 )
@@ -309,7 +316,7 @@ def tile_decoderblock_pb_k_kernel(
             out=h_codes[:].bitcast(FP8X4), scales=h_scales[:], in_=h_grouped[:]
         )
         permute_words(1)
-        for s in range(PASSES + 4):
+        for s in range(PASSES + 5):
             if s < PASSES:
                 first_product(s)
                 bias_relu(s)
@@ -319,14 +326,14 @@ def tile_decoderblock_pb_k_kernel(
                 make_pivot()
             if s + 2 < PASSES:
                 permute_words(s + 2)
-            if (s + 4) % (PLANES * ROUND) == 0 and (s + 4) // (PLANES * ROUND) < CHUNKS:
-                permute_scales((s + 4) // (PLANES * ROUND))
+            if (s + 2) % (PLANES * ROUND) == 0 and (s + 2) // (PLANES * ROUND) < CHUNKS:
+                permute_scales((s + 2) // (PLANES * ROUND))
             if 0 <= s - 1 < PASSES:
                 interleave(s - 1)
             if 0 <= s - 2 < PASSES:
                 quantise(s - 2)
-            if 0 <= s - 4 < PASSES:
-                second_product(s - 4)
+            if 0 <= s - 5 < PASSES:
+                second_product(s - 5)
 
         t_all = keep.tile([P, TOKEN_TILES, D], F32)
         square = keep.tile([P, TOKEN_TILES, D], F32)

@@ -80,21 +80,18 @@ def tile_decoderblock_pb_k_kernel(
         w1_planes_rest = keep.tile([P, rest_cols], U8, align_bytes=64)
         nc.vector.memset(w1_planes_rest[:].bitcast(I32), 0)
 
-        def load_w1_scales(planes, cols):
-            for quadrant in range(4):
-                nc.sync.dma_start(
-                    out=planes[32 * quadrant : 32 * quadrant + 4 * PLANES, :].bitcast(I32),
-                    in_=w_ff1_scales[0, 4 * quadrant : 4 * quadrant + 4, :]
-                    .rearrange("r (j c) -> j r c", j=PLANES)[:, :, cols]
-                    .bitcast(I32),
-                )
+        def load_w1_scales(planes, cols, quadrant):
+            nc.sync.dma_start(
+                out=planes[32 * quadrant : 32 * quadrant + 4 * PLANES, :].bitcast(I32),
+                in_=w_ff1_scales[0, 4 * quadrant : 4 * quadrant + 4, :]
+                .rearrange("r (j c) -> j r c", j=PLANES)[:, :, cols]
+                .bitcast(I32),
+            )
 
-        load_w1_scales(w1_planes_first, slice(0, chunk_cols))
+        for quadrant in range(4):
+            load_w1_scales(w1_planes_first, slice(0, chunk_cols), quadrant)
         load_w1(order[0], 1)
-
         load_w1(order[1], 1)
-        load_w1(first_pass_of(1), ROUND)
-        load_w1(first_pass_of(2), ROUND)
 
         ident_f32 = keep.tile([P, P], F32)
         make_identity(nc, ident_f32[:])
@@ -111,29 +108,45 @@ def tile_decoderblock_pb_k_kernel(
             nc.gpsimd.memset(planes[:].rearrange("p c n -> p (c n)").bitcast(I32), 0)
             w2_planes.append(planes)
 
-        def load_w2_scales(chunk):
-            for c in range(ROUND):
-                for quadrant in range(4):
-                    nc.sync.dma_start(
-                        out=w2_planes[chunk][
-                            32 * quadrant : 32 * quadrant + 4 * PLANES, c, :
-                        ].bitcast(I32),
-                        in_=w_ff2_scales[
-                            chunk * ROUND + c : PASSES : PER_PLANE,
-                            4 * quadrant : 4 * quadrant + 4,
-                            :,
-                        ].bitcast(I32),
-                    )
+        def load_w2_scales(chunk, c, quadrant):
+            nc.sync.dma_start(
+                out=w2_planes[chunk][32 * quadrant : 32 * quadrant + 4 * PLANES, c, :].bitcast(I32),
+                in_=w_ff2_scales[
+                    chunk * ROUND + c : PASSES : PER_PLANE,
+                    4 * quadrant : 4 * quadrant + 4,
+                    :,
+                ].bitcast(I32),
+            )
 
-        load_w2_scales(0)
+        small = [(0, c, quadrant) for c in range(ROUND) for quadrant in range(4)]
+        small += [(None, 0, quadrant) for quadrant in range(4)]
+        small += [
+            (chunk, c, quadrant)
+            for chunk in range(1, CHUNKS)
+            for c in range(ROUND)
+            for quadrant in range(4)
+        ]
+
+        def load_small(count):
+            for chunk, c, quadrant in small[:count]:
+                if chunk is None:
+                    load_w1_scales(
+                        w1_planes_rest, slice(chunk_cols, CHUNKS * chunk_cols), quadrant
+                    )
+                else:
+                    load_w2_scales(chunk, c, quadrant)
+            small[:count] = []
+
+        load_w1(first_pass_of(1), ROUND)
+        load_small(3)
+        load_w1(first_pass_of(2), ROUND)
+        load_small(5)
         for r in range(ROUNDS):
             load_w2(first_pass_of(r), ROUND)
+            load_small(2)
             if r + 3 < ROUNDS:
                 load_w1(first_pass_of(r + 3), ROUND)
-            if r == 0:
-                load_w1_scales(w1_planes_rest, slice(chunk_cols, CHUNKS * chunk_cols))
-            if r % PLANES == 1 and r // PLANES + 1 < CHUNKS:
-                load_w2_scales(r // PLANES + 1)
+                load_small(2)
 
         neg_average = keep.tile([P, P], F32)
         nc.gpsimd.memset(neg_average[:], -1.0 / (TOKENS * D))

@@ -252,10 +252,10 @@ def tile_decoderblock_pb_k_kernel(
             g = order[s]
             codes = work.tile([P, K_PASS], U32, tag="w1_codes", align_bytes=64)
             nc.vector.tensor_copy(
-                out=codes[:].bitcast(I32).rearrange("p (t c i) -> p c t i", t=PACK, i=4),
+                out=codes[:].bitcast(I32).rearrange("p (t m) -> p m t", t=PACK),
                 in_=w1_words[:, g * K_PASS : (g + 1) * K_PASS]
                 .bitcast(I32)
-                .rearrange("p (c i t) -> p c t i", t=PACK, i=4),
+                .rearrange("p (m t) -> p m t", t=PACK),
             )
             w1_codes_of[s] = codes
 
@@ -279,33 +279,46 @@ def tile_decoderblock_pb_k_kernel(
                     )
                 x_of[(s, half)] = x
 
+        def tokens_of(s):
+            if s == PASSES - 1:
+                return [token_tile(i) for i in range(TOKEN_TILES)]
+            return [slice(0, TOKENS)]
+
+        def words_of(tokens):
+            return slice(tokens.start * PACK, tokens.stop * PACK)
+
         def bias_relu(s):
             g = order[s]
             a = work.tile([P, PACK, TOKENS], BF16, tag="a")
-            for t in range(PACK):
-                nc.scalar.activation(
-                    out=a[:, t, :],
-                    in_=x_of[(s, t // 2)][:, t % 2, :],
-                    func=ACT.Relu,
-                    bias=bias_col[:, g, t : t + 1],
-                    scale=1.0,
-                )
+            for tokens in tokens_of(s):
+                for t in range(PACK):
+                    nc.scalar.activation(
+                        out=a[:, t, tokens],
+                        in_=x_of[(s, t // 2)][:, t % 2, tokens],
+                        func=ACT.Relu,
+                        bias=bias_col[:, g, t : t + 1],
+                        scale=1.0,
+                    )
             a_of[s] = a
 
         def interleave(s):
             grouped = work.tile([P, TOKENS * PACK], BF16, tag="grouped", align_bytes=64)
-            nc.vector.tensor_copy(
-                out=grouped[:].rearrange("p (c i t) -> p c t i", t=PACK, i=4),
-                in_=a_of[s][:].rearrange("p t (c i) -> p c t i", i=4),
-            )
+            for tokens in tokens_of(s):
+                nc.vector.tensor_copy(
+                    out=grouped[:, words_of(tokens)].rearrange("p (c i t) -> p c t i", t=PACK, i=4),
+                    in_=a_of[s][:, :, tokens].rearrange("p t (c i) -> p c t i", i=4),
+                )
             grouped_of[s] = grouped
 
         def quantise(s):
             a_codes = work.tile([P, TOKENS], U32, tag="a_codes", align_bytes=64)
             a_scales = work.tile([P, TOKENS], U8, tag="a_scales", align_bytes=64)
-            nc.vector.quantize_mx(
-                out=a_codes[:].bitcast(FP8X4), scales=a_scales[:], in_=grouped_of[s][:]
-            )
+            for tokens in tokens_of(s):
+                nc.vector.quantize_mx(
+                    out=a_codes[:, tokens].bitcast(FP8X4),
+                    scales=a_scales[:, tokens],
+                    in_=grouped_of[s][:, words_of(tokens)],
+                )
             a_mx_of[s] = (a_codes, a_scales)
 
         def second_product(s):
@@ -341,16 +354,22 @@ def tile_decoderblock_pb_k_kernel(
                 permute_words(s + 2)
             if (s + 2) % (PLANES * ROUND) == 0 and (s + 2) // (PLANES * ROUND) < CHUNKS:
                 permute_scales((s + 2) // (PLANES * ROUND))
-            if 0 <= s - 1 < PASSES:
-                interleave(s - 1)
-            if 0 <= s - 2 < PASSES:
+            if s - 1 == PASSES - 1:
                 quantise(s - 2)
+                interleave(s - 1)
+                quantise(s - 1)
+            elif s < PASSES:
+                if s >= 1:
+                    interleave(s - 1)
+                if s >= 2:
+                    quantise(s - 2)
             if 0 <= s - 5 < PASSES:
                 second_product(s - 5)
 
         t_all = keep.tile([P, TOKEN_TILES, D], F32)
         square = keep.tile([P, TOKEN_TILES, D], F32)
-        sums = keep.tile([P, TOKEN_TILES, 2], F32)
+        t_sum = keep.tile([P, TOKEN_TILES], F32)
+        square_sum = keep.tile([P, TOKEN_TILES], F32)
         for i in range(TOKEN_TILES):
             nc.vector.scalar_tensor_tensor(
                 out=t_all[:, i, :],
@@ -359,7 +378,7 @@ def tile_decoderblock_pb_k_kernel(
                 in1=residual[:, i, :],
                 op0=ALU.mult,
                 op1=ALU.add,
-                accum_out=sums[:, i, 0:1],
+                accum_out=t_sum[:, i : i + 1],
             )
             nc.scalar.activation(
                 out=square[:, i, :],
@@ -367,27 +386,32 @@ def tile_decoderblock_pb_k_kernel(
                 func=ACT.Square,
                 bias=neg_pivot[:],
                 scale=1.0,
-                accum_out=sums[:, i, 1:2],
+                accum_out=square_sum[:, i : i + 1],
             )
-        moments = minus_average([sums[:, i, :] for i in range(TOKEN_TILES)])
+        minus_m = minus_average([t_sum[:, i : i + 1] for i in range(TOKEN_TILES)])
+        minus_square = minus_average([square_sum[:, i : i + 1] for i in range(TOKEN_TILES)])
         shift = keep.tile([P, 1], F32)
-        nc.vector.tensor_tensor(
-            out=shift[:], in0=moments[:, 0:1], in1=neg_pivot[:], op=ALU.subtract
-        )
-        neg_var = keep.tile([P, 1], F32)
+        nc.vector.tensor_tensor(out=shift[:], in0=minus_m, in1=neg_pivot[:], op=ALU.subtract)
+        shift_square = keep.tile([P, 1], F32)
         nc.vector.scalar_tensor_tensor(
-            out=neg_var[:],
+            out=shift_square[:],
             in0=shift[:],
             scalar=shift[:],
-            in1=moments[:, 1:2],
+            in1=eps_col[:],
             op0=ALU.mult,
-            op1=ALU.add,
+            op1=ALU.subtract,
         )
+        known = keep.tile([P, 1], F32)
+        nc.vector.tensor_scalar_mul(known[:], shift_square[:], -1.0)
         neg_mean = keep.tile([P, 1], F32)
-        nc.vector.tensor_copy(out=neg_mean[:], in_=moments[:, 0:1])
+        nc.vector.tensor_copy(out=neg_mean[:], in_=minus_m)
         inv_std = keep.tile([P, 1], F32)
         nc.scalar.activation(
-            out=inv_std[:], in_=neg_var[:], func=ACT.Abs_reciprocal_sqrt, bias=eps_col[:], scale=-1.0
+            out=inv_std[:],
+            in_=minus_square,
+            func=ACT.Abs_reciprocal_sqrt,
+            bias=known[:],
+            scale=-1.0,
         )
         y = keep.tile([P, TOKEN_TILES, D], F32)
         for i in range(TOKEN_TILES):

@@ -38,6 +38,7 @@ def tile_decoderblock_pb_k_kernel(
     nc = tc.nc
     with ExitStack() as ctx:
         keep = ctx.enter_context(tc.tile_pool(name="keep", bufs=1))
+        w1_work = ctx.enter_context(tc.tile_pool(name="w1_work", bufs=4))
         work = ctx.enter_context(tc.tile_pool(name="work", bufs=6))
         psum_ff = ctx.enter_context(tc.psum_pool(name="psum_ff", bufs=1))
         psum_x = ctx.enter_context(tc.psum_pool(name="psum_x", bufs=6))
@@ -118,8 +119,8 @@ def tile_decoderblock_pb_k_kernel(
                 ].bitcast(I32),
             )
 
-        small = [(0, c, quadrant) for c in range(ROUND) for quadrant in range(4)]
-        small += [(None, 0, quadrant) for quadrant in range(4)]
+        small = [(None, 0, quadrant) for quadrant in range(4)]
+        small += [(0, c, quadrant) for c in range(ROUND) for quadrant in range(4)]
         small += [
             (chunk, c, quadrant)
             for chunk in range(1, CHUNKS)
@@ -138,14 +139,16 @@ def tile_decoderblock_pb_k_kernel(
             small[:count] = []
 
         load_w1(first_pass_of(1), ROUND)
-        load_small(3)
+        load_small(4)
         load_w1(first_pass_of(2), ROUND)
-        load_small(5)
+        load_small(4)
+        load_w1(first_pass_of(3), ROUND)
+        load_small(4)
         for r in range(ROUNDS):
             load_w2(first_pass_of(r), ROUND)
             load_small(2)
-            if r + 3 < ROUNDS:
-                load_w1(first_pass_of(r + 3), ROUND)
+            if r + 4 < ROUNDS:
+                load_w1(first_pass_of(r + 4), ROUND)
                 load_small(2)
 
         neg_average = keep.tile([P, P], F32)
@@ -248,16 +251,17 @@ def tile_decoderblock_pb_k_kernel(
             )
             w1_scales_of[chunk] = scales
 
-        def permute_words(s):
+        def permute_words(s, count):
             g = order[s]
-            codes = work.tile([P, K_PASS], U32, tag="w1_codes", align_bytes=64)
+            codes = w1_work.tile([P, ROUND, K_PASS], U32, tag="w1_codes", align_bytes=64)
             nc.vector.tensor_copy(
-                out=codes[:].bitcast(I32).rearrange("p (t m) -> p m t", t=PACK),
-                in_=w1_words[:, g * K_PASS : (g + 1) * K_PASS]
+                out=codes[:, 0:count, :].bitcast(I32).rearrange("p c (t m) -> p c m t", t=PACK),
+                in_=w1_words[:, g * K_PASS : (g + count) * K_PASS]
                 .bitcast(I32)
-                .rearrange("p (m t) -> p m t", t=PACK),
+                .rearrange("p (c m t) -> p c m t", t=PACK, m=P),
             )
-            w1_codes_of[s] = codes
+            for j in range(count):
+                w1_codes_of[s + j] = codes[:, j, :]
 
         def first_product(s):
             g = order[s]
@@ -279,18 +283,16 @@ def tile_decoderblock_pb_k_kernel(
                     )
                 x_of[(s, half)] = x
 
-        def tokens_of(s):
-            if s == PASSES - 1:
-                return [token_tile(i) for i in range(TOKEN_TILES)]
-            return [slice(0, TOKENS)]
-
         def words_of(tokens):
             return slice(tokens.start * PACK, tokens.stop * PACK)
 
         def bias_relu(s):
             g = order[s]
             a = work.tile([P, PACK, TOKENS], BF16, tag="a")
-            for tokens in tokens_of(s):
+            pieces = [slice(0, TOKENS)]
+            if s == PASSES - 1:
+                pieces = [token_tile(i) for i in range(TOKEN_TILES)]
+            for tokens in pieces:
                 for t in range(PACK):
                     nc.scalar.activation(
                         out=a[:, t, tokens],
@@ -300,26 +302,27 @@ def tile_decoderblock_pb_k_kernel(
                         scale=1.0,
                     )
             a_of[s] = a
+            grouped_of[s] = work.tile(
+                [P, TOKENS * PACK], BF16, tag="grouped", align_bytes=64, name="grouped"
+            )
+            a_mx_of[s] = (
+                work.tile([P, TOKENS], U32, tag="a_codes", align_bytes=64, name="a_codes"),
+                work.tile([P, TOKENS], U8, tag="a_scales", align_bytes=64, name="a_scales"),
+            )
 
-        def interleave(s):
-            grouped = work.tile([P, TOKENS * PACK], BF16, tag="grouped", align_bytes=64)
-            for tokens in tokens_of(s):
-                nc.vector.tensor_copy(
-                    out=grouped[:, words_of(tokens)].rearrange("p (c i t) -> p c t i", t=PACK, i=4),
-                    in_=a_of[s][:, :, tokens].rearrange("p t (c i) -> p c t i", i=4),
-                )
-            grouped_of[s] = grouped
+        def interleave(copy, s, tokens):
+            copy(
+                out=grouped_of[s][:, words_of(tokens)].rearrange("p (c i t) -> p c t i", t=PACK, i=4),
+                in_=a_of[s][:, :, tokens].rearrange("p t (c i) -> p c t i", i=4),
+            )
 
-        def quantise(s):
-            a_codes = work.tile([P, TOKENS], U32, tag="a_codes", align_bytes=64)
-            a_scales = work.tile([P, TOKENS], U8, tag="a_scales", align_bytes=64)
-            for tokens in tokens_of(s):
-                nc.vector.quantize_mx(
-                    out=a_codes[:, tokens].bitcast(FP8X4),
-                    scales=a_scales[:, tokens],
-                    in_=grouped_of[s][:, words_of(tokens)],
-                )
-            a_mx_of[s] = (a_codes, a_scales)
+        def quantise(s, tokens):
+            a_codes, a_scales = a_mx_of[s]
+            nc.vector.quantize_mx(
+                out=a_codes[:, tokens].bitcast(FP8X4),
+                scales=a_scales[:, tokens],
+                in_=grouped_of[s][:, words_of(tokens)],
+            )
 
         def second_product(s):
             g = order[s]
@@ -337,11 +340,13 @@ def tile_decoderblock_pb_k_kernel(
                 )
 
         permute_scales(0)
-        permute_words(0)
+        permute_words(0, 1)
         nc.vector.quantize_mx(
             out=h_codes[:].bitcast(FP8X4), scales=h_scales[:], in_=h_grouped[:]
         )
-        permute_words(1)
+        permute_words(1, 1)
+        permute_words(2, ROUND)
+        permute_scales(1)
         for s in range(PASSES + 5):
             if s < PASSES:
                 first_product(s)
@@ -350,19 +355,20 @@ def tile_decoderblock_pb_k_kernel(
                 add_residual(s - 2)
             if s == 4:
                 make_pivot()
-            if s + 2 < PASSES:
-                permute_words(s + 2)
-            if (s + 2) % (PLANES * ROUND) == 0 and (s + 2) // (PLANES * ROUND) < CHUNKS:
-                permute_scales((s + 2) // (PLANES * ROUND))
-            if s - 1 == PASSES - 1:
-                quantise(s - 2)
-                interleave(s - 1)
-                quantise(s - 1)
-            elif s < PASSES:
-                if s >= 1:
-                    interleave(s - 1)
-                if s >= 2:
-                    quantise(s - 2)
+            if 1 <= s < PASSES:
+                interleave(nc.vector.tensor_copy, s - 1, slice(0, TOKENS))
+            if 2 <= s <= PASSES:
+                quantise(s - 2, slice(0, TOKENS))
+            if s == PASSES:
+                halves = [token_tile(i) for i in range(TOKEN_TILES)]
+                interleave(nc.vector.tensor_copy, s - 1, halves[0])
+                interleave(nc.scalar.copy, s - 1, halves[1])
+                quantise(s - 1, halves[0])
+                quantise(s - 1, halves[1])
+            if s % ROUND == 1 and s + 3 < PASSES:
+                permute_words(s + 3, ROUND)
+            if s % (PLANES * ROUND) == 5 and s > PLANES * ROUND and s + 3 < PASSES:
+                permute_scales((s + 3) // (PLANES * ROUND))
             if 0 <= s - 5 < PASSES:
                 second_product(s - 5)
 

@@ -27,6 +27,7 @@ PER_PLANE = PASSES // PLANES
 ROUND = 2
 ROUNDS = PASSES // ROUND
 CHUNKS = PER_PLANE // ROUND
+SHARED = 10
 EPS = 1e-5
 
 FLOPS = 2 * TOKENS * D * F * 2
@@ -49,17 +50,9 @@ def tile_decoderblock_pb_k_kernel(
 
         order = [first_pass_of(r) + j for r in range(ROUNDS) for j in range(ROUND)]
 
-        eps_col = keep.tile([P, 1], F32)
-        nc.vector.memset(eps_col[:], EPS)
-
         h_tok = keep.tile([P, TOKEN_TILES, D], BF16)
-        nc.sync.dma_start(out=h_tok[:], in_=h2.rearrange("i p d -> p i d"))
-
-        bias_rows = keep.tile([P, K_PASS], BF16)
-        nc.vector.memset(bias_rows[:], 0.0)
-        nc.sync.dma_start(
-            out=bias_rows[0:PASSES, :], in_=b_ff1.rearrange("(g c) -> g c", c=K_PASS)
-        )
+        for i in range(TOKEN_TILES):
+            nc.sync.dma_start(out=h_tok[:, i, :], in_=h2[i])
 
         w1_words = keep.tile([P, F], U32, align_bytes=64)
         w2_words = keep.tile([P, PASSES, D], U32, align_bytes=64)
@@ -77,7 +70,11 @@ def tile_decoderblock_pb_k_kernel(
         chunk_cols = ROUND * K_PASS
         rest_cols = (CHUNKS - 1) * chunk_cols
         w1_planes_first = keep.tile([P, chunk_cols], U8, align_bytes=64)
-        nc.vector.memset(w1_planes_first[:].bitcast(I32), 0)
+        nc.gpsimd.memset(w1_planes_first[:].bitcast(I32), 0)
+        eps_col = keep.tile([P, 1], F32)
+        nc.vector.memset(eps_col[:], EPS)
+        bias_rows = keep.tile([P, K_PASS], BF16)
+        nc.vector.memset(bias_rows[:], 0.0)
         w1_planes_rest = keep.tile([P, rest_cols], U8, align_bytes=64)
         nc.vector.memset(w1_planes_rest[:].bitcast(I32), 0)
 
@@ -92,6 +89,11 @@ def tile_decoderblock_pb_k_kernel(
         for quadrant in range(4):
             load_w1_scales(w1_planes_first, slice(0, chunk_cols), quadrant)
         load_w1(order[0], 1)
+
+        nc.sync.dma_start(
+            out=bias_rows[0:PASSES, :], in_=b_ff1.rearrange("(g c) -> g c", c=K_PASS)
+        )
+
         load_w1(order[1], 1)
 
         ident_f32 = keep.tile([P, P], F32)
@@ -159,18 +161,26 @@ def tile_decoderblock_pb_k_kernel(
         def token_tile(i):
             return slice(i * P, (i + 1) * P)
 
-        hT = psum_x.tile([P, HALVES, TOKENS], F32, tag="x")
+        hT = []
         for i in range(TOKEN_TILES):
+            bank = psum_x.tile([P, HALVES, P], F32, tag="x")
             h_halves = h_tok[:, i, :].bitcast(F32)
             for u in range(HALVES):
                 nc.tensor.transpose(
-                    hT[:, u, token_tile(i)], h_halves[:, u : D // PAIR : HALVES], ident_f32[:]
+                    bank[:, u, :], h_halves[:, u : D // PAIR : HALVES], ident_f32[:]
                 )
+            hT.append(bank)
         h_grouped = keep.tile([P, TOKENS * PACK], BF16, align_bytes=64)
-        nc.scalar.copy(
-            out=h_grouped[:].bitcast(F32).rearrange("p (t u) -> p t u", u=HALVES),
-            in_=hT[:].rearrange("p u t -> p t u"),
-        )
+
+        def regroup_h(copy, i):
+            copy(
+                out=h_grouped[:, i * D : (i + 1) * D]
+                .bitcast(F32)
+                .rearrange("p (t u) -> p t u", u=HALVES),
+                in_=hT[i][:].rearrange("p u t -> p t u"),
+            )
+
+        regroup_h(nc.scalar.copy, 0)
         h_codes = keep.tile([P, TOKENS], U32, align_bytes=64)
         h_scales = keep.tile([P, TOKENS], U8, align_bytes=64)
 
@@ -237,19 +247,23 @@ def tile_decoderblock_pb_k_kernel(
         grouped_of = {}
         a_mx_of = {}
 
-        def permute_scales(chunk):
-            if chunk == 0:
-                raw = w1_planes_first[:]
-            else:
-                raw = w1_planes_rest[:, (chunk - 1) * chunk_cols : chunk * chunk_cols]
-            scales = keep.tile(
+        for chunk in range(CHUNKS):
+            w1_scales_of[chunk] = keep.tile(
                 [P, chunk_cols], U8, align_bytes=64, name="w1_scales%d" % chunk
             )
+
+        def permute_scales(chunk, first=0, count=ROUND):
+            raw, start = w1_planes_first[:], first * K_PASS
+            if chunk > 0:
+                raw, start = w1_planes_rest[:], (chunk - 1) * chunk_cols + first * K_PASS
             nc.vector.tensor_copy(
-                out=scales[:].rearrange("p (c t m) -> p c m t", t=PACK, m=P),
-                in_=raw.rearrange("p (c m t) -> p c m t", t=PACK, m=P),
+                out=w1_scales_of[chunk][:, first * K_PASS : (first + count) * K_PASS].rearrange(
+                    "p (c t m) -> p c m t", t=PACK, m=P
+                ),
+                in_=raw[:, start : start + count * K_PASS].rearrange(
+                    "p (c m t) -> p c m t", t=PACK, m=P
+                ),
             )
-            w1_scales_of[chunk] = scales
 
         def permute_words(s, count):
             g = order[s]
@@ -339,28 +353,34 @@ def tile_decoderblock_pb_k_kernel(
                     stop=(s == PASSES - 1),
                 )
 
-        permute_scales(0)
+        permute_scales(0, 0, 1)
+        regroup_h(nc.vector.tensor_copy, 1)
         permute_words(0, 1)
         nc.vector.quantize_mx(
             out=h_codes[:].bitcast(FP8X4), scales=h_scales[:], in_=h_grouped[:]
         )
+        permute_scales(0, 1, 1)
         permute_words(1, 1)
         permute_words(2, ROUND)
         permute_scales(1)
+        halves = [token_tile(i) for i in range(TOKEN_TILES)]
         for s in range(PASSES + 5):
             if s < PASSES:
                 first_product(s)
                 bias_relu(s)
             if s in (2, 3):
                 add_residual(s - 2)
-            if s == 4:
+            if s == 8:
                 make_pivot()
             if 1 <= s < PASSES:
-                interleave(nc.vector.tensor_copy, s - 1, slice(0, TOKENS))
+                if s % SHARED == 0:
+                    interleave(nc.vector.tensor_copy, s - 1, halves[0])
+                    interleave(nc.scalar.copy, s - 1, halves[1])
+                else:
+                    interleave(nc.vector.tensor_copy, s - 1, slice(0, TOKENS))
             if 2 <= s <= PASSES:
                 quantise(s - 2, slice(0, TOKENS))
             if s == PASSES:
-                halves = [token_tile(i) for i in range(TOKEN_TILES)]
                 interleave(nc.vector.tensor_copy, s - 1, halves[0])
                 interleave(nc.scalar.copy, s - 1, halves[1])
                 quantise(s - 1, halves[0])

from contextlib import ExitStack

import concourse.mybir as mybir
from concourse.masks import make_identity

F32 = mybir.dt.float32
BF16 = mybir.dt.bfloat16
I32 = mybir.dt.int32
U32 = mybir.dt.uint32
U8 = mybir.dt.uint8
FP8X4 = mybir.dt.float8_e4m3fn_x4
ALU = mybir.AluOpType
ACT = mybir.ActivationFunctionType

P = 128
PACK = 4
K_PASS = P * PACK
HALVES = 2
PAIR = 2
TOKEN_TILES = 2
TOKENS = TOKEN_TILES * P
D = 512
F = 16384
PASSES = F // K_PASS
PLANES = 4
PER_PLANE = PASSES // PLANES
ROUND = 2
ROUNDS = PASSES // ROUND
CHUNKS = PER_PLANE // ROUND
SHARED = 10
EPS = 1e-5

FLOPS = 2 * TOKENS * D * F * 2


def tile_decoderblock_pb_k_kernel(
    tc, h2, w_ff1_words, w_ff1_scales, b_ff1, w_ff2_words, w_ff2_scales, b_ff2, out
):
    nc = tc.nc
    with ExitStack() as ctx:
        keep = ctx.enter_context(tc.tile_pool(name="keep", bufs=1))
        w1_work = ctx.enter_context(tc.tile_pool(name="w1_work", bufs=4))
        work = ctx.enter_context(tc.tile_pool(name="work", bufs=6))
        psum_ff = ctx.enter_context(tc.psum_pool(name="psum_ff", bufs=1))
        psum_x = ctx.enter_context(tc.psum_pool(name="psum_x", bufs=6))
        ctx.enter_context(tc.manual_schedule())

        def first_pass_of(r):
            return PER_PLANE * (r % PLANES) + ROUND * (r // PLANES)

        order = [first_pass_of(r) + j for r in range(ROUNDS) for j in range(ROUND)]

        h_tok = keep.tile([P, TOKEN_TILES, D], BF16)
        for i in range(TOKEN_TILES):
            nc.sync.dma_start(out=h_tok[:, i, :], in_=h2[i])

        w1_words = keep.tile([P, F], U32, align_bytes=64)
        w2_words = keep.tile([P, PASSES, D], U32, align_bytes=64)
        w1_dram = w_ff1_words[0].rearrange("p n t -> p (n t)").bitcast(I32)
        w2_dram = w_ff2_words.rearrange("g p n t -> p g (n t)").bitcast(I32)

        def load_w1(g, count):
            cols = slice(g * K_PASS, (g + count) * K_PASS)
            nc.sync.dma_start(out=w1_words[:, cols].bitcast(I32), in_=w1_dram[:, cols])

        def load_w2(g, count):
            some = slice(g, g + count)
            nc.sync.dma_start(out=w2_words[:, some, :].bitcast(I32), in_=w2_dram[:, some, :])

        chunk_cols = ROUND * K_PASS
        rest_cols = (CHUNKS - 1) * chunk_cols
        w1_planes_first = keep.tile([P, chunk_cols], U8, align_bytes=64)
        nc.gpsimd.memset(w1_planes_first[:].bitcast(I32), 0)
        eps_col = keep.tile([P, 1], F32)
        nc.vector.memset(eps_col[:], EPS)
        bias_rows = keep.tile([P, K_PASS], BF16)
        nc.vector.memset(bias_rows[:], 0.0)
        w1_planes_rest = keep.tile([P, rest_cols], U8, align_bytes=64)
        nc.vector.memset(w1_planes_rest[:].bitcast(I32), 0)

        def load_w1_scales(planes, cols, quadrant):
            nc.sync.dma_start(
                out=planes[32 * quadrant : 32 * quadrant + 4 * PLANES, :].bitcast(I32),
                in_=w_ff1_scales[0, 4 * quadrant : 4 * quadrant + 4, :]
                .rearrange("r (j c) -> j r c", j=PLANES)[:, :, cols]
                .bitcast(I32),
            )

        for quadrant in range(4):
            load_w1_scales(w1_planes_first, slice(0, chunk_cols), quadrant)
        load_w1(order[0], 1)

        nc.sync.dma_start(
            out=bias_rows[0:PASSES, :], in_=b_ff1.rearrange("(g c) -> g c", c=K_PASS)
        )

        load_w1(order[1], 1)

        ident_f32 = keep.tile([P, P], F32)
        make_identity(nc, ident_f32[:])
        ident_bf16 = keep.tile([P, P], BF16)
        make_identity(nc, ident_bf16[:])
        b2_rows = keep.tile([P, D], BF16)
        nc.gpsimd.memset(b2_rows[:], 0.0)
        nc.gpsimd.dma_start(out=b2_rows[0:1, :], in_=b_ff2.rearrange("(o c) -> o c", o=1))
        w2_planes = []
        for chunk in range(CHUNKS):
            planes = keep.tile(
                [P, ROUND, D], U8, align_bytes=64, name="w2_planes%d" % chunk
            )
            nc.gpsimd.memset(planes[:].rearrange("p c n -> p (c n)").bitcast(I32), 0)
            w2_planes.append(planes)

        def load_w2_scales(chunk, c, quadrant):
            nc.sync.dma_start(
                out=w2_planes[chunk][32 * quadrant : 32 * quadrant + 4 * PLANES, c, :].bitcast(I32),
                in_=w_ff2_scales[
                    chunk * ROUND + c : PASSES : PER_PLANE,
                    4 * quadrant : 4 * quadrant + 4,
                    :,
                ].bitcast(I32),
            )

        small = [(None, 0, quadrant) for quadrant in range(4)]
        small += [(0, c, quadrant) for c in range(ROUND) for quadrant in range(4)]
        small += [
            (chunk, c, quadrant)
            for chunk in range(1, CHUNKS)
            for c in range(ROUND)
            for quadrant in range(4)
        ]

        def load_small(count):
            for chunk, c, quadrant in small[:count]:
                if chunk is None:
                    load_w1_scales(
                        w1_planes_rest, slice(chunk_cols, CHUNKS * chunk_cols), quadrant
                    )
                else:
                    load_w2_scales(chunk, c, quadrant)
            small[:count] = []

        load_w1(first_pass_of(1), ROUND)
        load_small(4)
        load_w1(first_pass_of(2), ROUND)
        load_small(4)
        load_w1(first_pass_of(3), ROUND)
        load_small(4)
        for r in range(ROUNDS):
            load_w2(first_pass_of(r), ROUND)
            load_small(2)
            if r + 4 < ROUNDS:
                load_w1(first_pass_of(r + 4), ROUND)
                load_small(2)

        neg_average = keep.tile([P, P], F32)
        nc.gpsimd.memset(neg_average[:], -1.0 / (TOKENS * D))
        warm = keep.tile([P, 1], F32)
        nc.scalar.activation(out=warm[:], in_=eps_col[:], func=ACT.Abs_reciprocal_sqrt)

        def token_tile(i):
            return slice(i * P, (i + 1) * P)

        hT = []
        for i in range(TOKEN_TILES):
            bank = psum_x.tile([P, HALVES, P], F32, tag="x")
            h_halves = h_tok[:, i, :].bitcast(F32)
            for u in range(HALVES):
                nc.tensor.transpose(
                    bank[:, u, :], h_halves[:, u : D // PAIR : HALVES], ident_f32[:]
                )
            hT.append(bank)
        h_grouped = keep.tile([P, TOKENS * PACK], BF16, align_bytes=64)

        def regroup_h(copy, i):
            copy(
                out=h_grouped[:, i * D : (i + 1) * D]
                .bitcast(F32)
                .rearrange("p (t u) -> p t u", u=HALVES),
                in_=hT[i][:].rearrange("p u t -> p t u"),
            )

        regroup_h(nc.scalar.copy, 0)
        h_codes = keep.tile([P, TOKENS], U32, align_bytes=64)
        h_scales = keep.tile([P, TOKENS], U8, align_bytes=64)

        biasT = psum_x.tile([P, HALVES, P], F32, tag="x")
        bias_halves = bias_rows[:].bitcast(F32)
        for u in range(HALVES):
            nc.tensor.transpose(
                biasT[:, u, :], bias_halves[:, u : K_PASS // PAIR : HALVES], ident_f32[:]
            )
        bias_col = keep.tile([P, PASSES, PACK], F32)
        nc.scalar.copy(
            out=bias_col[:].rearrange("p g (u e) -> p u g e", u=HALVES),
            in_=biasT[:].bitcast(BF16).rearrange("p u (g e) -> p u g e", e=PAIR)[:, :, 0:PASSES, :],
        )

        residual = keep.tile([P, TOKEN_TILES, D], F32)
        residual_sum = keep.tile([P, TOKEN_TILES], F32)

        def add_residual(i):
            bank = psum_x.tile([P, D], F32, tag="x")
            nc.tensor.matmul(
                out=bank[:], lhsT=ident_bf16[:], rhs=h_tok[:, i, :], start=True, stop=False
            )
            nc.tensor.matmul(
                out=bank[:],
                lhsT=ident_bf16[:, 0:1].to_broadcast([P, P]),
                rhs=b2_rows[:],
                start=False,
                stop=True,
            )
            nc.scalar.activation(
                out=residual[:, i, :],
                in_=bank[:],
                func=ACT.Identity,
                accum_out=residual_sum[:, i : i + 1],
            )

        def minus_average(columns):
            width = columns[0].shape[1]
            bank = psum_x.tile([P, K_PASS], F32, tag="x")
            for j, column in enumerate(columns):
                nc.tensor.matmul(
                    out=bank[:, 0:width],
                    lhsT=neg_average[:],
                    rhs=column,
                    start=(j == 0),
                    stop=(j == len(columns) - 1),
                )
            return bank[:, 0:width]

        neg_pivot = keep.tile([P, 1], F32)

        def make_pivot():
            minus_c = minus_average([residual_sum[:, i : i + 1] for i in range(TOKEN_TILES)])
            nc.scalar.copy(out=neg_pivot[:], in_=minus_c)

        ff = [
            psum_ff.tile([P, D], F32, name="ff%d" % i, tag="ff%d" % i) for i in range(TOKEN_TILES)
        ]
        w1_scales_of = {}
        w1_codes_of = {}
        x_of = {}
        a_of = {}
        grouped_of = {}
        a_mx_of = {}

        for chunk in range(CHUNKS):
            w1_scales_of[chunk] = keep.tile(
                [P, chunk_cols], U8, align_bytes=64, name="w1_scales%d" % chunk
            )

        def permute_scales(chunk, first=0, count=ROUND):
            raw, start = w1_planes_first[:], first * K_PASS
            if chunk > 0:
                raw, start = w1_planes_rest[:], (chunk - 1) * chunk_cols + first * K_PASS
            nc.vector.tensor_copy(
                out=w1_scales_of[chunk][:, first * K_PASS : (first + count) * K_PASS].rearrange(
                    "p (c t m) -> p c m t", t=PACK, m=P
                ),
                in_=raw[:, start : start + count * K_PASS].rearrange(
                    "p (c m t) -> p c m t", t=PACK, m=P
                ),
            )

        def permute_words(s, count):
            g = order[s]
            codes = w1_work.tile([P, ROUND, K_PASS], U32, tag="w1_codes", align_bytes=64)
            nc.vector.tensor_copy(
                out=codes[:, 0:count, :].bitcast(I32).rearrange("p c (t m) -> p c m t", t=PACK),
                in_=w1_words[:, g * K_PASS : (g + count) * K_PASS]
                .bitcast(I32)
                .rearrange("p (c m t) -> p c m t", t=PACK, m=P),
            )
            for j in range(count):
                w1_codes_of[s + j] = codes[:, j, :]

        def first_product(s):
            g = order[s]
            plane = g // PER_PLANE
            scales = w1_scales_of[s // (PLANES * ROUND)]
            for half in range(2):
                x = psum_x.tile([P, 2, TOKENS], F32, tag="x")
                for j in range(2):
                    t = 2 * half + j
                    col = (g % ROUND) * K_PASS + t * P
                    nc.tensor.matmul_mx(
                        out=x[:, j, :],
                        lhsT=w1_codes_of[s][:, t * P : (t + 1) * P].bitcast(FP8X4),
                        lhsT_scale=scales[4 * plane : P, col : col + P],
                        rhs=h_codes[:].bitcast(FP8X4),
                        rhs_scale=h_scales[:],
                        start=True,
                        stop=True,
                    )
                x_of[(s, half)] = x

        def words_of(tokens):
            return slice(tokens.start * PACK, tokens.stop * PACK)

        def bias_relu(s):
            g = order[s]
            a = work.tile([P, PACK, TOKENS], BF16, tag="a")
            pieces = [slice(0, TOKENS)]
            if s == PASSES - 1:
                pieces = [token_tile(i) for i in range(TOKEN_TILES)]
            for tokens in pieces:
                for t in range(PACK):
                    nc.scalar.activation(
                        out=a[:, t, tokens],
                        in_=x_of[(s, t // 2)][:, t % 2, tokens],
                        func=ACT.Relu,
                        bias=bias_col[:, g, t : t + 1],
                        scale=1.0,
                    )
            a_of[s] = a
            grouped_of[s] = work.tile(
                [P, TOKENS * PACK], BF16, tag="grouped", align_bytes=64, name="grouped"
            )
            a_mx_of[s] = (
                work.tile([P, TOKENS], U32, tag="a_codes", align_bytes=64, name="a_codes"),
                work.tile([P, TOKENS], U8, tag="a_scales", align_bytes=64, name="a_scales"),
            )

        def interleave(copy, s, tokens):
            copy(
                out=grouped_of[s][:, words_of(tokens)].rearrange("p (c i t) -> p c t i", t=PACK, i=4),
                in_=a_of[s][:, :, tokens].rearrange("p t (c i) -> p c t i", i=4),
            )

        def quantise(s, tokens):
            a_codes, a_scales = a_mx_of[s]
            nc.vector.quantize_mx(
                out=a_codes[:, tokens].bitcast(FP8X4),
                scales=a_scales[:, tokens],
                in_=grouped_of[s][:, words_of(tokens)],
            )

        def second_product(s):
            g = order[s]
            plane = g // PER_PLANE
            a_codes, a_scales = a_mx_of[s]
            for i in range(TOKEN_TILES):
                nc.tensor.matmul_mx(
                    out=ff[i][:],
                    lhsT=a_codes[:, token_tile(i)].bitcast(FP8X4),
                    lhsT_scale=a_scales[:, token_tile(i)],
                    rhs=w2_words[:, g, :].bitcast(FP8X4),
                    rhs_scale=w2_planes[s // (PLANES * ROUND)][4 * plane : P, g % ROUND, :],
                    start=(s == 0),
                    stop=(s == PASSES - 1),
                )

        permute_scales(0, 0, 1)
        regroup_h(nc.vector.tensor_copy, 1)
        permute_words(0, 1)
        nc.vector.quantize_mx(
            out=h_codes[:].bitcast(FP8X4), scales=h_scales[:], in_=h_grouped[:]
        )
        permute_scales(0, 1, 1)
        permute_words(1, 1)
        permute_words(2, ROUND)
        permute_scales(1)
        halves = [token_tile(i) for i in range(TOKEN_TILES)]
        for s in range(PASSES + 5):
            if s < PASSES:
                first_product(s)
                bias_relu(s)
            if s in (2, 3):
                add_residual(s - 2)
            if s == 8:
                make_pivot()
            if 1 <= s < PASSES:
                if s % SHARED == 0:
                    interleave(nc.vector.tensor_copy, s - 1, halves[0])
                    interleave(nc.scalar.copy, s - 1, halves[1])
                else:
                    interleave(nc.vector.tensor_copy, s - 1, slice(0, TOKENS))
            if 2 <= s <= PASSES:
                quantise(s - 2, slice(0, TOKENS))
            if s == PASSES:
                interleave(nc.vector.tensor_copy, s - 1, halves[0])
                interleave(nc.scalar.copy, s - 1, halves[1])
                quantise(s - 1, halves[0])
                quantise(s - 1, halves[1])
            if s % ROUND == 1 and s + 3 < PASSES:
                permute_words(s + 3, ROUND)
            if s % (PLANES * ROUND) == 5 and s > PLANES * ROUND and s + 3 < PASSES:
                permute_scales((s + 3) // (PLANES * ROUND))
            if 0 <= s - 5 < PASSES:
                second_product(s - 5)

        t_all = keep.tile([P, TOKEN_TILES, D], F32)
        square = keep.tile([P, TOKEN_TILES, D], F32)
        t_sum = keep.tile([P, TOKEN_TILES], F32)
        square_sum = keep.tile([P, TOKEN_TILES], F32)
        for i in range(TOKEN_TILES):
            nc.vector.scalar_tensor_tensor(
                out=t_all[:, i, :],
                in0=ff[i][:],
                scalar=1.0,
                in1=residual[:, i, :],
                op0=ALU.mult,
                op1=ALU.add,
                accum_out=t_sum[:, i : i + 1],
            )
            nc.scalar.activation(
                out=square[:, i, :],
                in_=t_all[:, i, :],
                func=ACT.Square,
                bias=neg_pivot[:],
                scale=1.0,
                accum_out=square_sum[:, i : i + 1],
            )
        minus_m = minus_average([t_sum[:, i : i + 1] for i in range(TOKEN_TILES)])
        minus_square = minus_average([square_sum[:, i : i + 1] for i in range(TOKEN_TILES)])
        shift = keep.tile([P, 1], F32)
        nc.vector.tensor_tensor(out=shift[:], in0=minus_m, in1=neg_pivot[:], op=ALU.subtract)
        shift_square = keep.tile([P, 1], F32)
        nc.vector.scalar_tensor_tensor(
            out=shift_square[:],
            in0=shift[:],
            scalar=shift[:],
            in1=eps_col[:],
            op0=ALU.mult,
            op1=ALU.subtract,
        )
        known = keep.tile([P, 1], F32)
        nc.vector.tensor_scalar_mul(known[:], shift_square[:], -1.0)
        neg_mean = keep.tile([P, 1], F32)
        nc.vector.tensor_copy(out=neg_mean[:], in_=minus_m)
        inv_std = keep.tile([P, 1], F32)
        nc.scalar.activation(
            out=inv_std[:],
            in_=minus_square,
            func=ACT.Abs_reciprocal_sqrt,
            bias=known[:],
            scale=-1.0,
        )
        y = keep.tile([P, TOKEN_TILES, D], F32)
        for i in range(TOKEN_TILES):
            nc.vector.tensor_scalar(
                out=y[:, i, :],
                in0=t_all[:, i, :],
                scalar1=neg_mean[:],
                scalar2=inv_std[:],
                op0=ALU.add,
                op1=ALU.mult,
            )
            nc.sync.dma_start(out=out[i], in_=y[:, i, :])
